import numpy as np
import ml_dtypes


def mxq(x, axis, fmt="e4m3"):
    dtype, down = {"e4m3": (ml_dtypes.float8_e4m3fn, 7), "e5m2": (ml_dtypes.float8_e5m2, 14)}[fmt]
    v = np.moveaxis(np.asarray(x, np.float32).astype(ml_dtypes.bfloat16).astype(np.float64), axis, -1)
    blocks = v.reshape(v.shape[:-1] + (-1, 32))
    amax = np.abs(blocks).max(-1, keepdims=True)
    byte = np.maximum(np.where(amax > 0, np.frexp(amax)[1] - 1 + 127, 0) - down, 1)
    scale = np.exp2(byte - 127.0)
    codes = (blocks / scale).astype(np.float32).astype(dtype).astype(np.float64)
    return np.moveaxis((codes * scale).reshape(v.shape), -1, axis)


WIDE = False


def mx_kscale(k):
    if not WIDE:
        return np.ones(k)
    levels = np.array([10, -10, 5, -5, 0])
    a = np.random.permutation(np.resize(levels, k // 512 * 4)).reshape(k // 512, 4)
    idx = np.arange(k)
    return np.exp2(a[idx // 512, idx % 128 // 32])


BF16 = ml_dtypes.bfloat16


def bf(x):
    return np.asarray(x, np.float32).astype(BF16)


def f64(x):
    return np.asarray(x).astype(np.float64)


B, S, D, H, DFF = 4, 1024, 256, 8, 1024


def wave(v, w1, w2):
    return w1 * np.sin(v) + w2 * np.cos(v)


def setup_inputs():
    n = np.random.standard_normal
    s = mx_kscale(DFF)
    u = n((B, S, DFF))
    return {
        "h1": bf((np.sin(u) + np.cos(u)) * s),
        "x1": bf(n((B, S, D)) * 1.2),
        "ffn_w2": bf(n((DFF, DFF)) / np.sqrt(DFF) / s[None, :]),
        "ffn_b2": bf(n(DFF) * 0.2),
        "ffn_a2w1": bf(1.2 + 0.1 * n(1)),
        "ffn_a2w2": bf(0.8 + 0.1 * n(1)),
        "ffn_w3": bf(n((D, DFF)) / np.sqrt(DFF)),
        "ffn_b3": bf(n(D) * 0.2),
    }


def reference(h1, x1, ffn_w2, ffn_b2, ffn_a2w1, ffn_a2w2, ffn_w3, ffn_b3):
    u2 = (mxq(f64(h1), 2, "e4m3") @ mxq(f64(ffn_w2), 1, "e4m3").T) + f64(ffn_b2)
    h2 = wave(u2, f64(ffn_a2w1), f64(ffn_a2w2))
    ffn_out = (mxq(h2, 2, "e4m3") @ mxq(f64(ffn_w3), 1, "e4m3").T) + f64(ffn_b3)
    return f64(x1) + ffn_out

@@ -1,0 +1,337 @@
+import math
+from contextlib import ExitStack
+
+import concourse.mybir as mybir
+from concourse.masks import make_identity
+
+F32 = mybir.dt.float32
+BF16 = mybir.dt.bfloat16
+U32 = mybir.dt.uint32
+U8 = mybir.dt.uint8
+FP8X4 = mybir.dt.float8_e4m3fn_x4
+ALU = mybir.AluOpType
+ACT = mybir.ActivationFunctionType
+
+P = 128
+PACK = 4
+TOKENS = 4 * 1024
+HIDDEN = 1024
+MODEL = 256
+PASSES = HIDDEN // (P * PACK)
+CHUNK = 512
+ROW_TILES = CHUNK // P
+N_CHUNKS = TOKENS // CHUNK
+N_HALVES = N_CHUNKS * PASSES
+WORDS = P * PACK // 2
+
+TWO_PI = 2.0 * math.pi
+ROUND_MAGIC = 1.5 * 2.0**23
+TINY = 1e-30
+PHASE_STEPS = 3
+
+FLOPS = 2 * TOKENS * HIDDEN * HIDDEN + 2 * TOKENS * HIDDEN * MODEL
+
+
+def k_onto_partitions(nc, banks, stage, tag, identity, copy, rows, n_tiles, g):
+    words = rows.bitcast(F32)
+    grouped = stage.tile([P, n_tiles * P * PACK], BF16, tag=tag, align_bytes=64)
+    pairs = grouped[:].bitcast(F32).rearrange("p (r u) -> p r u", u=2)
+    for first in range(0, n_tiles, 2):
+        bank = banks.tile([P, 2, 2 * P], F32, tag="bank")
+        for u in range(2):
+            for i in range(2):
+                w0 = g * WORDS + u * P
+                nc.tensor.transpose(
+                    out=bank[:, u, i * P : (i + 1) * P],
+                    in_=words[:, first + i, w0 : w0 + P],
+                    identity=identity,
+                )
+        copy(out=pairs[:, first * P : (first + 2) * P, :], in_=bank[:].rearrange("p u r -> p r u"))
+    return grouped
+
+
+def quantise(nc, grouped, g, codes, scales):
+    nc.vector.quantize_mx(out=codes[:, g, :].bitcast(FP8X4), scales=scales[:, g, :], in_=grouped[:])
+
+
+def wave_constants(nc, keep, w1_dram, w2_dram):
+    w1_bf = keep.tile([P, 1], BF16)
+    w2_bf = keep.tile([P, 1], BF16)
+    nc.sync.dma_start(out=w1_bf[:], in_=w1_dram.partition_broadcast(P))
+    nc.sync.dma_start(out=w2_bf[:], in_=w2_dram.partition_broadcast(P))
+    gains = keep.tile([P, 2], F32)
+    nc.gpsimd.tensor_copy(out=gains[:, 0:1], in_=w1_bf[:])
+    nc.gpsimd.tensor_copy(out=gains[:, 1:2], in_=w2_bf[:])
+
+    minus_half = keep.tile([P, 1], F32)
+    w1_sq = keep.tile([P, 1], F32)
+    amp_sq = keep.tile([P, 1], F32)
+    inv_amp = keep.tile([P, 1], F32)
+    nc.gpsimd.memset(minus_half[:], -0.5)
+    nc.gpsimd.tensor_scalar(
+        out=w1_sq[:], in0=gains[:, 0:1], scalar1=gains[:, 0:1], scalar2=TINY,
+        op0=ALU.mult, op1=ALU.add,
+    )
+    nc.gpsimd.tensor_scalar(
+        out=amp_sq[:], in0=gains[:, 1:2], scalar1=gains[:, 1:2], scalar2=w1_sq[:, 0:1],
+        op0=ALU.mult, op1=ALU.add,
+    )
+    nc.gpsimd.tensor_tensor(out=inv_amp[:], in0=amp_sq[:], in1=minus_half[:], op=ALU.pow)
+
+    half = keep.tile([P, 1], F32)
+    coef = keep.tile([P, 1], F32)
+    ab = keep.tile([P, 2], F32)
+    nc.gpsimd.tensor_scalar(
+        out=half[:], in0=gains[:, 1:2], scalar1=0.0, scalar2=0.5, op0=ALU.is_ge, op1=ALU.subtract
+    )
+    nc.gpsimd.tensor_scalar(
+        out=coef[:], in0=half[:], scalar1=-2.0, scalar2=inv_amp[:, 0:1], op0=ALU.mult, op1=ALU.mult
+    )
+    nc.gpsimd.tensor_scalar(
+        out=ab[:], in0=gains[:], scalar1=coef[:, 0:1], scalar2=1.0, op0=ALU.mult, op1=ALU.mult
+    )
+
+    angles = keep.tile([P, 2], F32)
+    cos_sin = keep.tile([P, 2], F32)
+    partial = keep.tile([P, 1], F32)
+    psi = angles[:, 1:2]
+    nc.gpsimd.tensor_copy(out=psi, in_=ab[:, 0:1])
+
+    def cos_and_sin_of_psi():
+        nc.gpsimd.tensor_scalar(
+            out=angles[:, 0:1], in0=psi, scalar1=0.5 * math.pi, scalar2=1.0, op0=ALU.add, op1=ALU.mult
+        )
+        nc.scalar.activation(out=cos_sin[:], in_=angles[:], func=ACT.Sin)
+
+    for step in range(PHASE_STEPS):
+        cos_and_sin_of_psi()
+        nc.gpsimd.tensor_scalar(
+            out=partial[:], in0=cos_sin[:, 0:1], scalar1=ab[:, 0:1], scalar2=psi,
+            op0=ALU.mult, op1=ALU.add,
+        )
+        nc.gpsimd.tensor_scalar(
+            out=psi, in0=cos_sin[:, 1:2], scalar1=ab[:, 1:2], scalar2=partial[:, 0:1],
+            op0=ALU.mult, op1=ALU.add,
+        )
+
+    quarter_turn = keep.tile([P, 1], F32)
+    phase_turns = keep.tile([P, 1], F32)
+    nc.gpsimd.tensor_scalar(
+        out=quarter_turn[:], in0=half[:], scalar1=0.5, scalar2=1.0, op0=ALU.mult, op1=ALU.mult
+    )
+    nc.gpsimd.tensor_scalar(
+        out=phase_turns[:], in0=psi, scalar1=1.0 / TWO_PI, scalar2=quarter_turn[:, 0:1],
+        op0=ALU.mult, op1=ALU.add,
+    )
+
+    signed = keep.tile([P, 2], F32)
+    w1_part = keep.tile([P, 1], F32)
+    amp = keep.tile([P, 1], F32)
+    nc.gpsimd.tensor_scalar(
+        out=signed[:], in0=gains[:], scalar1=half[:, 0:1], scalar2=2.0, op0=ALU.mult, op1=ALU.mult
+    )
+    cos_and_sin_of_psi()
+    nc.gpsimd.tensor_scalar(
+        out=w1_part[:], in0=cos_sin[:, 1:2], scalar1=signed[:, 0:1], scalar2=1.0,
+        op0=ALU.mult, op1=ALU.mult,
+    )
+    nc.gpsimd.tensor_scalar(
+        out=amp[:], in0=cos_sin[:, 0:1], scalar1=signed[:, 1:2], scalar2=w1_part[:, 0:1],
+        op0=ALU.mult, op1=ALU.subtract,
+    )
+    return amp, phase_turns
+
+
+def tile_transreachencoderlayer_pb_t_kernel(
+    tc, h1, x1, ffn_w2, ffn_b2, ffn_a2w1, ffn_a2w2, ffn_w3, ffn_b3, out
+):
+    nc = tc.nc
+    h1_chunks = h1.flatten_outer_dims().rearrange("(c p i) k -> c p i k", p=P, i=ROW_TILES)
+    x1_chunks = x1.flatten_outer_dims().rearrange("(c p i) d -> c p i d", p=P, i=ROW_TILES)
+    out_chunks = out.flatten_outer_dims().rearrange("(c p i) d -> c p i d", p=P, i=ROW_TILES)
+
+    with ExitStack() as pools:
+        keep = pools.enter_context(tc.tile_pool(name="keep", bufs=1))
+        stage = pools.enter_context(tc.tile_pool(name="stage", bufs=2))
+        loads = pools.enter_context(tc.tile_pool(name="loads", bufs=3))
+        wave = pools.enter_context(tc.tile_pool(name="wave", bufs=3))
+        banks = pools.enter_context(tc.psum_pool(name="banks", bufs=2))
+        u2_banks = pools.enter_context(tc.psum_pool(name="u2_banks", bufs=4))
+        out_banks = pools.enter_context(tc.psum_pool(name="out_banks", bufs=2))
+
+        amp, phase_turns = wave_constants(nc, keep, ffn_a2w1, ffn_a2w2)
+        b2_rows = keep.tile([P, 2 * P], BF16)
+        nc.vector.memset(b2_rows[:], 0.0)
+        nc.sync.dma_start(out=b2_rows[0:4, :], in_=ffn_b2.rearrange("(a w) -> a w", a=4))
+        b3_all = keep.tile([P, MODEL], BF16)
+        nc.sync.dma_start(out=b3_all[:], in_=ffn_b3.partition_broadcast(P))
+
+        w2_raw = keep.tile([P, PASSES * PACK, HIDDEN], BF16)
+        w3_raw = keep.tile([P, MODEL // P, HIDDEN], BF16)
+        h1_raw = {}
+        x1_raw = {}
+
+        def load_w2(g2):
+            nc.sync.dma_start(
+                out=w2_raw[:, g2 * PACK : (g2 + 1) * PACK, :].rearrange("m (a e) k -> m a (e k)", e=2),
+                in_=ffn_w2[g2 * CHUNK : (g2 + 1) * CHUNK, :].rearrange("(a m e) k -> m a (e k)", m=P, e=2),
+            )
+
+        def load_chunk(c):
+            h1_raw[c] = loads.tile([P, ROW_TILES, HIDDEN], BF16, tag="h1_raw", name="h1_raw")
+            nc.sync.dma_start(out=h1_raw[c][:], in_=h1_chunks[c])
+            x1_raw[c] = loads.tile([P, ROW_TILES, MODEL], BF16, tag="x1_raw", name="x1_raw")
+            nc.sync.dma_start(out=x1_raw[c][:], in_=x1_chunks[c])
+
+        load_w2(0)
+        load_chunk(0)
+        load_w2(1)
+        nc.sync.dma_start(out=w3_raw[:], in_=ffn_w3.rearrange("(i p) k -> p i k", p=P))
+        load_chunk(1)
+
+        identity = keep.tile([P, P], F32)
+        make_identity(nc, identity[:])
+
+        b2_bank = banks.tile([P, 2, 2 * P], F32, tag="bank")
+        nc.tensor.transpose(out=b2_bank[:, 0, 0:P], in_=b2_rows[:].bitcast(F32), identity=identity[:])
+        b2_words = keep.tile([P, PASSES * PACK // 2], F32)
+        nc.vector.tensor_copy(out=b2_words[:], in_=b2_bank[:, 0, 0 : PASSES * PACK // 2])
+        b2_cols = keep.tile([P, PASSES * PACK], F32)
+        nc.vector.tensor_copy(out=b2_cols[:], in_=b2_words[:].bitcast(BF16))
+        turn_bias = keep.tile([P, PASSES * PACK], F32)
+        nc.vector.tensor_scalar(
+            out=turn_bias[:], in0=b2_cols[:], scalar1=1.0 / TWO_PI, scalar2=phase_turns[:, 0:1],
+            op0=ALU.mult, op1=ALU.add,
+        )
+
+        w2_codes = keep.tile([P, PASSES, HIDDEN], U32, align_bytes=64)
+        w2_scales = keep.tile([P, PASSES, HIDDEN], U8, align_bytes=64)
+        w3_codes = keep.tile([P, PASSES, MODEL], U32, align_bytes=64)
+        w3_scales = keep.tile([P, PASSES, MODEL], U8, align_bytes=64)
+
+        def prepare_weight(rows, n_tiles, tag, codes, scales):
+            for g in range(PASSES):
+                grouped = k_onto_partitions(
+                    nc, banks, stage, tag, identity[:], nc.vector.tensor_copy, rows, n_tiles, g
+                )
+                quantise(nc, grouped, g, codes, scales)
+
+        h1_codes = {}
+        h1_scales = {}
+
+        def group_h1(c, g):
+            if g == 0:
+                h1_codes[c] = stage.tile([P, PASSES, CHUNK], U32, tag="h1_codes", name="h1_codes", align_bytes=64)
+                h1_scales[c] = stage.tile([P, PASSES, CHUNK], U8, tag="h1_scales", name="h1_scales", align_bytes=64)
+            return k_onto_partitions(
+                nc, banks, stage, "h1_grouped", identity[:], nc.scalar.copy, h1_raw[c][:], ROW_TILES, g
+            )
+
+        def w2_half(g2):
+            cols = slice(g2 * CHUNK, (g2 + 1) * CHUNK)
+            prepare_weight(
+                w2_raw[:, g2 * PACK : (g2 + 1) * PACK, :], PACK, "w2_grouped",
+                w2_codes[:, :, cols], w2_scales[:, :, cols],
+            )
+
+        w2_half(0)
+        for g in range(PASSES):
+            quantise(nc, group_h1(0, g), g, h1_codes[0], h1_scales[0])
+        w2_half(1)
+        prepare_weight(w3_raw[:], MODEL // P, "w3_grouped", w3_codes[:], w3_scales[:])
+
+        turns_of = {}
+        h2_codes = {}
+        h2_scales = {}
+        residual = {}
+
+        def first_matmul(i):
+            c, g2 = divmod(i, PASSES)
+            turns_of[i] = wave.tile([P, PACK, CHUNK], F32, tag="turns", name="turns")
+            for t in range(PACK):
+                j = g2 * PACK + t
+                acc = u2_banks.tile([P, CHUNK], F32, tag="u2")
+                for g in range(PASSES):
+                    nc.tensor.matmul_mx(
+                        out=acc[:],
+                        lhsT=w2_codes[:, g, j * P : (j + 1) * P].bitcast(FP8X4),
+                        lhsT_scale=w2_scales[:, g, j * P : (j + 1) * P],
+                        rhs=h1_codes[c][:, g, :].bitcast(FP8X4),
+                        rhs_scale=h1_scales[c][:, g, :],
+                        start=(g == 0),
+                        stop=(g == PASSES - 1),
+                    )
+                nc.scalar.activation(
+                    out=turns_of[i][:, t, :], in_=acc[:], func=ACT.Identity,
+                    bias=turn_bias[:, j : j + 1], scale=1.0 / TWO_PI,
+                )
+
+        def drop_whole_turns(i):
+            turns = turns_of[i]
+            whole = wave.tile([P, PACK, CHUNK], F32, tag="whole", bufs=2)
+            nc.vector.tensor_scalar(
+                out=whole[:], in0=turns[:], scalar1=ROUND_MAGIC, scalar2=ROUND_MAGIC,
+                op0=ALU.add, op1=ALU.subtract,
+            )
+            nc.vector.tensor_tensor(out=turns[:], in0=turns[:], in1=whole[:], op=ALU.subtract)
+
+        def wave_and_quantise(i):
+            c, g2 = divmod(i, PASSES)
+            turns = turns_of[i]
+            if g2 == 0:
+                h2_codes[c] = stage.tile([P, PASSES, CHUNK], U32, tag="h2_codes", name="h2_codes", align_bytes=64)
+                h2_scales[c] = stage.tile([P, PASSES, CHUNK], U8, tag="h2_scales", name="h2_scales", align_bytes=64)
+            nc.scalar.activation(out=turns[:], in_=turns[:], func=ACT.Sin, scale=TWO_PI)
+            h2_grouped = stage.tile([P, CHUNK, PACK], BF16, tag="h2_grouped", align_bytes=64)
+            nc.vector.tensor_scalar(
+                out=h2_grouped[:], in0=turns[:].rearrange("p t n -> p n t"),
+                scalar1=amp[:, 0:1], scalar2=None, op0=ALU.mult,
+            )
+            nc.vector.quantize_mx(
+                out=h2_codes[c][:, g2, :].bitcast(FP8X4), scales=h2_scales[c][:, g2, :],
+                in_=h2_grouped[:].rearrange("p n t -> p (n t)"),
+            )
+
+        def second_matmul(c):
+            result = loads.tile([P, ROW_TILES, MODEL], F32, tag="result", bufs=2)
+            for first in range(0, ROW_TILES, 2):
+                acc2 = out_banks.tile([P, 2, MODEL], F32, tag="acc2")
+                for i in range(2):
+                    tok = slice((first + i) * P, (first + i + 1) * P)
+                    for g2 in range(PASSES):
+                        nc.tensor.matmul_mx(
+                            out=acc2[:, i, :],
+                            lhsT=h2_codes[c][:, g2, tok].bitcast(FP8X4),
+                            lhsT_scale=h2_scales[c][:, g2, tok],
+                            rhs=w3_codes[:, g2, :].bitcast(FP8X4),
+                            rhs_scale=w3_scales[:, g2, :],
+                            start=(g2 == 0),
+                            stop=(g2 == PASSES - 1),
+                        )
+                nc.vector.tensor_tensor(
+                    out=result[:, first : first + 2, :], in0=acc2[:],
+                    in1=residual[c][:, first : first + 2, :], op=ALU.add,
+                )
+            nc.sync.dma_start(out=out_chunks[c], in_=result[:])
+
+        for i in range(N_HALVES + 2):
+            c, g2 = divmod(i, PASSES)
+            if i < N_HALVES:
+                first_matmul(i)
+            if i >= 3 and g2 == 1:
+                second_matmul(c - 1)
+            if i < N_HALVES:
+                if g2 == 0:
+                    if c + 2 < N_CHUNKS:
+                        load_chunk(c + 2)
+                    residual[c] = loads.tile([P, ROW_TILES, MODEL], F32, tag="residual", name="residual")
+                    nc.gpsimd.tensor_tensor(
+                        out=residual[c][:], in0=x1_raw[c][:],
+                        in1=b3_all[:].unsqueeze(1).to_broadcast([P, ROW_TILES, MODEL]), op=ALU.add,
+                    )
+                next_grouped = group_h1(c + 1, g2) if c + 1 < N_CHUNKS else None
+                drop_whole_turns(i)
+                if next_grouped is not None:
+                    quantise(nc, next_grouped, g2, h1_codes[c + 1], h1_scales[c + 1])
+            if 1 <= i <= N_HALVES:
+                wave_and_quantise(i - 1)

@@ -163,8 +163,9 @@ def tile_transreachencoderlayer_pb_t_kernel(
         b2_rows = keep.tile([P, 2 * P], BF16)
         nc.vector.memset(b2_rows[:], 0.0)
         nc.sync.dma_start(out=b2_rows[0:4, :], in_=ffn_b2.rearrange("(a w) -> a w", a=4))
-        b3_all = keep.tile([P, MODEL], BF16)
-        nc.sync.dma_start(out=b3_all[:], in_=ffn_b3.partition_broadcast(P))
+        b3_row = keep.tile([P, MODEL], BF16)
+        nc.vector.memset(b3_row[:], 0.0)
+        nc.sync.dma_start(out=b3_row[0:1, :], in_=ffn_b3.rearrange("(o d) -> o d", o=1))
 
         w2_raw = keep.tile([P, PASSES * PACK, HIDDEN], BF16)
         w3_raw = keep.tile([P, MODEL // P, HIDDEN], BF16)
@@ -191,6 +192,11 @@ def tile_transreachencoderlayer_pb_t_kernel(
 
         identity = keep.tile([P, P], F32)
         make_identity(nc, identity[:])
+        identity_bf = keep.tile([P, P], BF16)
+        make_identity(nc, identity_bf[:])
+        first_row = keep.tile([P, P], BF16)
+        nc.vector.memset(first_row[:], 0.0)
+        nc.vector.memset(first_row[0:1, :], 1.0)
 
         b2_bank = banks.tile([P, 2, 2 * P], F32, tag="bank")
         nc.tensor.transpose(out=b2_bank[:, 0, 0:P], in_=b2_rows[:].bitcast(F32), identity=identity[:])
@@ -292,6 +298,20 @@ def tile_transreachencoderlayer_pb_t_kernel(
                 in_=h2_grouped[:].rearrange("p n t -> p (n t)"),
             )
 
+        def residual_and_bias(c):
+            residual[c] = loads.tile([P, ROW_TILES, MODEL], F32, tag="residual", name="residual")
+            for first in range(0, ROW_TILES, 2):
+                bank = banks.tile([P, 2, MODEL], F32, tag="bank")
+                for i in range(2):
+                    nc.tensor.matmul(
+                        out=bank[:, i, :], lhsT=identity_bf[:], rhs=x1_raw[c][:, first + i, :],
+                        start=True, stop=False,
+                    )
+                    nc.tensor.matmul(
+                        out=bank[:, i, :], lhsT=first_row[:], rhs=b3_row[:], start=False, stop=True
+                    )
+                nc.scalar.copy(out=residual[c][:, first : first + 2, :], in_=bank[:])
+
         def second_matmul(c):
             result = loads.tile([P, ROW_TILES, MODEL], F32, tag="result", bufs=2)
             for first in range(0, ROW_TILES, 2):
@@ -324,11 +344,7 @@ def tile_transreachencoderlayer_pb_t_kernel(
                 if g2 == 0:
                     if c + 2 < N_CHUNKS:
                         load_chunk(c + 2)
-                    residual[c] = loads.tile([P, ROW_TILES, MODEL], F32, tag="residual", name="residual")
-                    nc.gpsimd.tensor_tensor(
-                        out=residual[c][:], in0=x1_raw[c][:],
-                        in1=b3_all[:].unsqueeze(1).to_broadcast([P, ROW_TILES, MODEL]), op=ALU.add,
-                    )
+                    residual_and_bias(c)
                 next_grouped = group_h1(c + 1, g2) if c + 1 < N_CHUNKS else None
                 drop_whole_turns(i)
                 if next_grouped is not None:

@@ -55,24 +55,27 @@ def quantise(nc, grouped, g, codes, scales):
 
 
 def wave_constants(nc, keep, w1_dram, w2_dram):
+    warm = keep.tile([P, 1], F32)
+    nc.vector.memset(warm[:], 0.0)
+    nc.scalar.activation(out=warm[:], in_=warm[:], func=ACT.Sin)
     w1_bf = keep.tile([P, 1], BF16)
     w2_bf = keep.tile([P, 1], BF16)
     nc.sync.dma_start(out=w1_bf[:], in_=w1_dram.partition_broadcast(P))
     nc.sync.dma_start(out=w2_bf[:], in_=w2_dram.partition_broadcast(P))
     gains = keep.tile([P, 2], F32)
-    nc.gpsimd.tensor_copy(out=gains[:, 0:1], in_=w1_bf[:])
-    nc.gpsimd.tensor_copy(out=gains[:, 1:2], in_=w2_bf[:])
+    nc.vector.tensor_copy(out=gains[:, 0:1], in_=w1_bf[:])
+    nc.vector.tensor_copy(out=gains[:, 1:2], in_=w2_bf[:])
 
     minus_half = keep.tile([P, 1], F32)
     w1_sq = keep.tile([P, 1], F32)
     amp_sq = keep.tile([P, 1], F32)
     inv_amp = keep.tile([P, 1], F32)
-    nc.gpsimd.memset(minus_half[:], -0.5)
-    nc.gpsimd.tensor_scalar(
+    nc.vector.memset(minus_half[:], -0.5)
+    nc.vector.tensor_scalar(
         out=w1_sq[:], in0=gains[:, 0:1], scalar1=gains[:, 0:1], scalar2=TINY,
         op0=ALU.mult, op1=ALU.add,
     )
-    nc.gpsimd.tensor_scalar(
+    nc.vector.tensor_scalar(
         out=amp_sq[:], in0=gains[:, 1:2], scalar1=gains[:, 1:2], scalar2=w1_sq[:, 0:1],
         op0=ALU.mult, op1=ALU.add,
     )
@@ -81,13 +84,13 @@ def wave_constants(nc, keep, w1_dram, w2_dram):
     half = keep.tile([P, 1], F32)
     coef = keep.tile([P, 1], F32)
     ab = keep.tile([P, 2], F32)
-    nc.gpsimd.tensor_scalar(
+    nc.vector.tensor_scalar(
         out=half[:], in0=gains[:, 1:2], scalar1=0.0, scalar2=0.5, op0=ALU.is_ge, op1=ALU.subtract
     )
-    nc.gpsimd.tensor_scalar(
+    nc.vector.tensor_scalar(
         out=coef[:], in0=half[:], scalar1=-2.0, scalar2=inv_amp[:, 0:1], op0=ALU.mult, op1=ALU.mult
     )
-    nc.gpsimd.tensor_scalar(
+    nc.vector.tensor_scalar(
         out=ab[:], in0=gains[:], scalar1=coef[:, 0:1], scalar2=1.0, op0=ALU.mult, op1=ALU.mult
     )
 
@@ -95,31 +98,31 @@ def wave_constants(nc, keep, w1_dram, w2_dram):
     cos_sin = keep.tile([P, 2], F32)
     partial = keep.tile([P, 1], F32)
     psi = angles[:, 1:2]
-    nc.gpsimd.tensor_copy(out=psi, in_=ab[:, 0:1])
+    nc.vector.tensor_copy(out=psi, in_=ab[:, 0:1])
 
     def cos_and_sin_of_psi():
-        nc.gpsimd.tensor_scalar(
+        nc.vector.tensor_scalar(
             out=angles[:, 0:1], in0=psi, scalar1=0.5 * math.pi, scalar2=1.0, op0=ALU.add, op1=ALU.mult
         )
         nc.scalar.activation(out=cos_sin[:], in_=angles[:], func=ACT.Sin)
 
     for step in range(PHASE_STEPS):
         cos_and_sin_of_psi()
-        nc.gpsimd.tensor_scalar(
+        nc.vector.tensor_scalar(
             out=partial[:], in0=cos_sin[:, 0:1], scalar1=ab[:, 0:1], scalar2=psi,
             op0=ALU.mult, op1=ALU.add,
         )
-        nc.gpsimd.tensor_scalar(
+        nc.vector.tensor_scalar(
             out=psi, in0=cos_sin[:, 1:2], scalar1=ab[:, 1:2], scalar2=partial[:, 0:1],
             op0=ALU.mult, op1=ALU.add,
         )
 
     quarter_turn = keep.tile([P, 1], F32)
     phase_turns = keep.tile([P, 1], F32)
-    nc.gpsimd.tensor_scalar(
+    nc.vector.tensor_scalar(
         out=quarter_turn[:], in0=half[:], scalar1=0.5, scalar2=1.0, op0=ALU.mult, op1=ALU.mult
     )
-    nc.gpsimd.tensor_scalar(
+    nc.vector.tensor_scalar(
         out=phase_turns[:], in0=psi, scalar1=1.0 / TWO_PI, scalar2=quarter_turn[:, 0:1],
         op0=ALU.mult, op1=ALU.add,
     )
@@ -127,15 +130,15 @@ def wave_constants(nc, keep, w1_dram, w2_dram):
     signed = keep.tile([P, 2], F32)
     w1_part = keep.tile([P, 1], F32)
     amp = keep.tile([P, 1], F32)
-    nc.gpsimd.tensor_scalar(
+    nc.vector.tensor_scalar(
         out=signed[:], in0=gains[:], scalar1=half[:, 0:1], scalar2=2.0, op0=ALU.mult, op1=ALU.mult
     )
     cos_and_sin_of_psi()
-    nc.gpsimd.tensor_scalar(
+    nc.vector.tensor_scalar(
         out=w1_part[:], in0=cos_sin[:, 1:2], scalar1=signed[:, 0:1], scalar2=1.0,
         op0=ALU.mult, op1=ALU.mult,
     )
-    nc.gpsimd.tensor_scalar(
+    nc.vector.tensor_scalar(
         out=amp[:], in0=cos_sin[:, 0:1], scalar1=signed[:, 1:2], scalar2=w1_part[:, 0:1],
         op0=ALU.mult, op1=ALU.subtract,
     )
@@ -152,12 +155,12 @@ def tile_transreachencoderlayer_pb_t_kernel(
 
     with ExitStack() as pools:
         keep = pools.enter_context(tc.tile_pool(name="keep", bufs=1))
-        stage = pools.enter_context(tc.tile_pool(name="stage", bufs=2))
+        stage = pools.enter_context(tc.tile_pool(name="stage", bufs=3))
         loads = pools.enter_context(tc.tile_pool(name="loads", bufs=3))
         wave = pools.enter_context(tc.tile_pool(name="wave", bufs=3))
-        banks = pools.enter_context(tc.psum_pool(name="banks", bufs=2))
+        banks = pools.enter_context(tc.psum_pool(name="banks", bufs=3))
         u2_banks = pools.enter_context(tc.psum_pool(name="u2_banks", bufs=4))
-        out_banks = pools.enter_context(tc.psum_pool(name="out_banks", bufs=2))
+        out_banks = pools.enter_context(tc.psum_pool(name="out_banks", bufs=1))
 
         amp, phase_turns = wave_constants(nc, keep, ffn_a2w1, ffn_a2w2)
         b2_rows = keep.tile([P, 2 * P], BF16)
@@ -178,17 +181,21 @@ def tile_transreachencoderlayer_pb_t_kernel(
                 in_=ffn_w2[g2 * CHUNK : (g2 + 1) * CHUNK, :].rearrange("(a m e) k -> m a (e k)", m=P, e=2),
             )
 
-        def load_chunk(c):
+        def load_h1(c):
             h1_raw[c] = loads.tile([P, ROW_TILES, HIDDEN], BF16, tag="h1_raw", name="h1_raw")
             nc.sync.dma_start(out=h1_raw[c][:], in_=h1_chunks[c])
+
+        def load_x1(c):
             x1_raw[c] = loads.tile([P, ROW_TILES, MODEL], BF16, tag="x1_raw", name="x1_raw")
             nc.sync.dma_start(out=x1_raw[c][:], in_=x1_chunks[c])
 
         load_w2(0)
-        load_chunk(0)
+        load_h1(0)
         load_w2(1)
+        load_h1(1)
+        load_x1(0)
         nc.sync.dma_start(out=w3_raw[:], in_=ffn_w3.rearrange("(i p) k -> p i k", p=P))
-        load_chunk(1)
+        load_h1(2)
 
         identity = keep.tile([P, P], F32)
         make_identity(nc, identity[:])
@@ -225,13 +232,20 @@ def tile_transreachencoderlayer_pb_t_kernel(
         h1_codes = {}
         h1_scales = {}
 
-        def group_h1(c, g):
+        h1_grouped = {}
+
+        def group_h1(q):
+            c, g = divmod(q, PASSES)
+            h1_grouped[q] = k_onto_partitions(
+                nc, banks, stage, "h1_grouped", identity[:], nc.scalar.copy, h1_raw[c][:], ROW_TILES, g
+            )
+
+        def quantise_h1(q):
+            c, g = divmod(q, PASSES)
             if g == 0:
                 h1_codes[c] = stage.tile([P, PASSES, CHUNK], U32, tag="h1_codes", name="h1_codes", align_bytes=64)
                 h1_scales[c] = stage.tile([P, PASSES, CHUNK], U8, tag="h1_scales", name="h1_scales", align_bytes=64)
-            return k_onto_partitions(
-                nc, banks, stage, "h1_grouped", identity[:], nc.scalar.copy, h1_raw[c][:], ROW_TILES, g
-            )
+            quantise(nc, h1_grouped[q], g, h1_codes[c], h1_scales[c])
 
         def w2_half(g2):
             cols = slice(g2 * CHUNK, (g2 + 1) * CHUNK)
@@ -240,13 +254,10 @@ def tile_transreachencoderlayer_pb_t_kernel(
                 w2_codes[:, :, cols], w2_scales[:, :, cols],
             )
 
-        w2_half(0)
-        for g in range(PASSES):
-            quantise(nc, group_h1(0, g), g, h1_codes[0], h1_scales[0])
-        w2_half(1)
-        prepare_weight(w3_raw[:], MODEL // P, "w3_grouped", w3_codes[:], w3_scales[:])
 
         turns_of = {}
+        whole_of = {}
+        h2_grouped = {}
         h2_codes = {}
         h2_scales = {}
         residual = {}
@@ -272,82 +283,108 @@ def tile_transreachencoderlayer_pb_t_kernel(
                     bias=turn_bias[:, j : j + 1], scale=1.0 / TWO_PI,
                 )
 
-        def drop_whole_turns(i):
-            turns = turns_of[i]
-            whole = wave.tile([P, PACK, CHUNK], F32, tag="whole", bufs=2)
+        def nearest_whole_turns(i):
+            whole_of[i] = wave.tile([P, PACK, CHUNK], F32, tag="whole", name="whole", bufs=2)
             nc.vector.tensor_scalar(
-                out=whole[:], in0=turns[:], scalar1=ROUND_MAGIC, scalar2=ROUND_MAGIC,
+                out=whole_of[i][:], in0=turns_of[i][:], scalar1=ROUND_MAGIC, scalar2=ROUND_MAGIC,
                 op0=ALU.add, op1=ALU.subtract,
             )
-            nc.vector.tensor_tensor(out=turns[:], in0=turns[:], in1=whole[:], op=ALU.subtract)
 
-        def wave_and_quantise(i):
+        def drop_whole_turns(i):
+            nc.vector.tensor_tensor(
+                out=turns_of[i][:], in0=turns_of[i][:], in1=whole_of[i][:], op=ALU.subtract
+            )
+
+        def sine(i):
+            nc.scalar.activation(out=turns_of[i][:], in_=turns_of[i][:], func=ACT.Sin, scale=TWO_PI)
+
+        def gain(i):
+            h2_grouped[i] = stage.tile([P, CHUNK, PACK], BF16, tag="h2_grouped", name="h2_grouped", align_bytes=64)
+            nc.vector.tensor_scalar(
+                out=h2_grouped[i][:], in0=turns_of[i][:].rearrange("p t n -> p n t"),
+                scalar1=amp[:, 0:1], scalar2=None, op0=ALU.mult,
+            )
+
+        def quantise_h2(i):
             c, g2 = divmod(i, PASSES)
-            turns = turns_of[i]
             if g2 == 0:
                 h2_codes[c] = stage.tile([P, PASSES, CHUNK], U32, tag="h2_codes", name="h2_codes", align_bytes=64)
                 h2_scales[c] = stage.tile([P, PASSES, CHUNK], U8, tag="h2_scales", name="h2_scales", align_bytes=64)
-            nc.scalar.activation(out=turns[:], in_=turns[:], func=ACT.Sin, scale=TWO_PI)
-            h2_grouped = stage.tile([P, CHUNK, PACK], BF16, tag="h2_grouped", align_bytes=64)
-            nc.vector.tensor_scalar(
-                out=h2_grouped[:], in0=turns[:].rearrange("p t n -> p n t"),
-                scalar1=amp[:, 0:1], scalar2=None, op0=ALU.mult,
-            )
             nc.vector.quantize_mx(
                 out=h2_codes[c][:, g2, :].bitcast(FP8X4), scales=h2_scales[c][:, g2, :],
-                in_=h2_grouped[:].rearrange("p n t -> p (n t)"),
+                in_=h2_grouped[i][:].rearrange("p n t -> p (n t)"),
             )
 
-        def residual_and_bias(c):
-            residual[c] = loads.tile([P, ROW_TILES, MODEL], F32, tag="residual", name="residual")
-            for first in range(0, ROW_TILES, 2):
-                bank = banks.tile([P, 2, MODEL], F32, tag="bank")
-                for i in range(2):
-                    nc.tensor.matmul(
-                        out=bank[:, i, :], lhsT=identity_bf[:], rhs=x1_raw[c][:, first + i, :],
-                        start=True, stop=False,
-                    )
-                    nc.tensor.matmul(
-                        out=bank[:, i, :], lhsT=first_row[:], rhs=b3_row[:], start=False, stop=True
-                    )
-                nc.scalar.copy(out=residual[c][:, first : first + 2, :], in_=bank[:])
-
-        def second_matmul(c):
-            result = loads.tile([P, ROW_TILES, MODEL], F32, tag="result", bufs=2)
-            for first in range(0, ROW_TILES, 2):
-                acc2 = out_banks.tile([P, 2, MODEL], F32, tag="acc2")
-                for i in range(2):
-                    tok = slice((first + i) * P, (first + i + 1) * P)
-                    for g2 in range(PASSES):
-                        nc.tensor.matmul_mx(
-                            out=acc2[:, i, :],
-                            lhsT=h2_codes[c][:, g2, tok].bitcast(FP8X4),
-                            lhsT_scale=h2_scales[c][:, g2, tok],
-                            rhs=w3_codes[:, g2, :].bitcast(FP8X4),
-                            rhs_scale=w3_scales[:, g2, :],
-                            start=(g2 == 0),
-                            stop=(g2 == PASSES - 1),
-                        )
-                nc.vector.tensor_tensor(
-                    out=result[:, first : first + 2, :], in0=acc2[:],
-                    in1=residual[c][:, first : first + 2, :], op=ALU.add,
+        def residual_and_bias(r):
+            c, first = r // 2, 2 * (r % 2)
+            residual[r] = loads.tile([P, 2, MODEL], F32, tag="residual", name="residual", bufs=5)
+            bank = banks.tile([P, 2, MODEL], F32, tag="bank")
+            for i in range(2):
+                nc.tensor.matmul(
+                    out=bank[:, i, :], lhsT=identity_bf[:], rhs=x1_raw[c][:, first + i, :],
+                    start=True, stop=False,
                 )
-            nc.sync.dma_start(out=out_chunks[c], in_=result[:])
+                nc.tensor.matmul(
+                    out=bank[:, i, :], lhsT=first_row[:], rhs=b3_row[:], start=False, stop=True
+                )
+            nc.scalar.copy(out=residual[r][:], in_=bank[:])
 
-        for i in range(N_HALVES + 2):
-            c, g2 = divmod(i, PASSES)
-            if i < N_HALVES:
-                first_matmul(i)
-            if i >= 3 and g2 == 1:
-                second_matmul(c - 1)
-            if i < N_HALVES:
-                if g2 == 0:
-                    if c + 2 < N_CHUNKS:
-                        load_chunk(c + 2)
-                    residual_and_bias(c)
-                next_grouped = group_h1(c + 1, g2) if c + 1 < N_CHUNKS else None
-                drop_whole_turns(i)
-                if next_grouped is not None:
-                    quantise(nc, next_grouped, g2, h1_codes[c + 1], h1_scales[c + 1])
-            if 1 <= i <= N_HALVES:
-                wave_and_quantise(i - 1)
+        def second_matmul(r):
+            c, first = r // 2, 2 * (r % 2)
+            acc2 = out_banks.tile([P, 2, MODEL], F32, tag="acc2")
+            for i in range(2):
+                tok = slice((first + i) * P, (first + i + 1) * P)
+                for g2 in range(PASSES):
+                    nc.tensor.matmul_mx(
+                        out=acc2[:, i, :],
+                        lhsT=h2_codes[c][:, g2, tok].bitcast(FP8X4),
+                        lhsT_scale=h2_scales[c][:, g2, tok],
+                        rhs=w3_codes[:, g2, :].bitcast(FP8X4),
+                        rhs_scale=w3_scales[:, g2, :],
+                        start=(g2 == 0),
+                        stop=(g2 == PASSES - 1),
+                    )
+            result = loads.tile([P, 2, MODEL], F32, tag="result")
+            nc.vector.tensor_tensor(out=result[:], in0=acc2[:], in1=residual[r][:], op=ALU.add)
+            nc.sync.dma_start(out=out_chunks[c][:, first : first + 2, :], in_=result[:])
+
+        w2_half(0)
+        group_h1(0)
+        group_h1(1)
+        load_h1(3)
+        quantise_h1(0)
+        quantise_h1(1)
+        first_matmul(0)
+        w2_half(1)
+        group_h1(2)
+        group_h1(3)
+        quantise_h1(2)
+        prepare_weight(w3_raw[:], MODEL // P, "w3_grouped", w3_codes[:], w3_scales[:])
+
+        with tc.manual_schedule():
+            for i in range(N_HALVES + 3):
+                if 1 <= i <= N_HALVES:
+                    sine(i - 1)
+                if 2 <= i <= N_HALVES + 1:
+                    quantise_h2(i - 2)
+                if i + 3 < N_HALVES:
+                    quantise_h1(i + 3)
+                if i + 1 < N_HALVES:
+                    first_matmul(i + 1)
+                if i < N_HALVES:
+                    nearest_whole_turns(i)
+                if i + 4 < N_HALVES:
+                    group_h1(i + 4)
+                if i < N_HALVES:
+                    residual_and_bias(i)
+                if i >= 3:
+                    second_matmul(i - 3)
+                if 1 <= i <= N_HALVES:
+                    gain(i - 1)
+                if i < N_HALVES:
+                    drop_whole_turns(i)
+                if i % 2 == 0:
+                    if i // 2 + 4 < N_CHUNKS:
+                        load_h1(i // 2 + 4)
+                    if i // 2 + 1 < N_CHUNKS:
+                        load_x1(i // 2 + 1)

@@ -18,15 +18,17 @@ TOKENS = 4 * 1024
 HIDDEN = 1024
 MODEL = 256
 PASSES = HIDDEN // (P * PACK)
+WORDS = P * PACK // 2
 CHUNK = 512
 ROW_TILES = CHUNK // P
+FEATURE_TILES = HIDDEN // P
 N_CHUNKS = TOKENS // CHUNK
-N_HALVES = N_CHUNKS * PASSES
-WORDS = P * PACK // 2
+UNITS = 2 * N_CHUNKS
 
 TWO_PI = 2.0 * math.pi
 ROUND_MAGIC = 1.5 * 2.0**23
 TINY = 1e-30
+SECOND_LAG = 4
 PHASE_STEPS = 3
 
 FLOPS = 2 * TOKENS * HIDDEN * HIDDEN + 2 * TOKENS * HIDDEN * MODEL
@@ -51,13 +53,14 @@ def k_onto_partitions(nc, banks, stage, tag, identity, copy, rows, n_tiles, g):
 
 
 def quantise(nc, grouped, g, codes, scales):
-    nc.vector.quantize_mx(out=codes[:, g, :].bitcast(FP8X4), scales=scales[:, g, :], in_=grouped[:])
+    nc.vector.quantize_mx(out=codes[:, g, :].bitcast(FP8X4), scales=scales[:, g, :], in_=grouped)
 
 
 def wave_constants(nc, keep, w1_dram, w2_dram):
     warm = keep.tile([P, 1], F32)
     nc.vector.memset(warm[:], 0.0)
     nc.scalar.activation(out=warm[:], in_=warm[:], func=ACT.Sin)
+
     w1_bf = keep.tile([P, 1], BF16)
     w2_bf = keep.tile([P, 1], BF16)
     nc.sync.dma_start(out=w1_bf[:], in_=w1_dram.partition_broadcast(P))
@@ -90,9 +93,7 @@ def wave_constants(nc, keep, w1_dram, w2_dram):
     nc.vector.tensor_scalar(
         out=coef[:], in0=half[:], scalar1=-2.0, scalar2=inv_amp[:, 0:1], op0=ALU.mult, op1=ALU.mult
     )
-    nc.vector.tensor_scalar(
-        out=ab[:], in0=gains[:], scalar1=coef[:, 0:1], scalar2=1.0, op0=ALU.mult, op1=ALU.mult
-    )
+    nc.vector.tensor_scalar(out=ab[:], in0=gains[:], scalar1=coef[:, 0:1], scalar2=None, op0=ALU.mult)
 
     angles = keep.tile([P, 2], F32)
     cos_sin = keep.tile([P, 2], F32)
@@ -102,11 +103,11 @@ def wave_constants(nc, keep, w1_dram, w2_dram):
 
     def cos_and_sin_of_psi():
         nc.vector.tensor_scalar(
-            out=angles[:, 0:1], in0=psi, scalar1=0.5 * math.pi, scalar2=1.0, op0=ALU.add, op1=ALU.mult
+            out=angles[:, 0:1], in0=psi, scalar1=0.5 * math.pi, scalar2=None, op0=ALU.add
         )
         nc.scalar.activation(out=cos_sin[:], in_=angles[:], func=ACT.Sin)
 
-    for step in range(PHASE_STEPS):
+    for repeat in range(PHASE_STEPS):
         cos_and_sin_of_psi()
         nc.vector.tensor_scalar(
             out=partial[:], in0=cos_sin[:, 0:1], scalar1=ab[:, 0:1], scalar2=psi,
@@ -119,9 +120,7 @@ def wave_constants(nc, keep, w1_dram, w2_dram):
 
     quarter_turn = keep.tile([P, 1], F32)
     phase_turns = keep.tile([P, 1], F32)
-    nc.vector.tensor_scalar(
-        out=quarter_turn[:], in0=half[:], scalar1=0.5, scalar2=1.0, op0=ALU.mult, op1=ALU.mult
-    )
+    nc.vector.tensor_scalar(out=quarter_turn[:], in0=half[:], scalar1=0.5, scalar2=None, op0=ALU.mult)
     nc.vector.tensor_scalar(
         out=phase_turns[:], in0=psi, scalar1=1.0 / TWO_PI, scalar2=quarter_turn[:, 0:1],
         op0=ALU.mult, op1=ALU.add,
@@ -135,8 +134,7 @@ def wave_constants(nc, keep, w1_dram, w2_dram):
     )
     cos_and_sin_of_psi()
     nc.vector.tensor_scalar(
-        out=w1_part[:], in0=cos_sin[:, 1:2], scalar1=signed[:, 0:1], scalar2=1.0,
-        op0=ALU.mult, op1=ALU.mult,
+        out=w1_part[:], in0=cos_sin[:, 1:2], scalar1=signed[:, 0:1], scalar2=None, op0=ALU.mult
     )
     nc.vector.tensor_scalar(
         out=amp[:], in0=cos_sin[:, 0:1], scalar1=signed[:, 1:2], scalar2=w1_part[:, 0:1],
@@ -159,26 +157,31 @@ def tile_transreachencoderlayer_pb_t_kernel(
         loads = pools.enter_context(tc.tile_pool(name="loads", bufs=3))
         wave = pools.enter_context(tc.tile_pool(name="wave", bufs=3))
         banks = pools.enter_context(tc.psum_pool(name="banks", bufs=3))
-        u2_banks = pools.enter_context(tc.psum_pool(name="u2_banks", bufs=4))
+        u2_banks = pools.enter_context(tc.psum_pool(name="u2_banks", bufs=PACK))
         out_banks = pools.enter_context(tc.psum_pool(name="out_banks", bufs=1))
 
         amp, phase_turns = wave_constants(nc, keep, ffn_a2w1, ffn_a2w2)
         b2_rows = keep.tile([P, 2 * P], BF16)
         nc.vector.memset(b2_rows[:], 0.0)
-        nc.sync.dma_start(out=b2_rows[0:4, :], in_=ffn_b2.rearrange("(a w) -> a w", a=4))
+        nc.sync.dma_start(
+            out=b2_rows[0 : FEATURE_TILES // 2, :],
+            in_=ffn_b2.rearrange("(a w) -> a w", a=FEATURE_TILES // 2),
+        )
         b3_row = keep.tile([P, MODEL], BF16)
         nc.vector.memset(b3_row[:], 0.0)
         nc.sync.dma_start(out=b3_row[0:1, :], in_=ffn_b3.rearrange("(o d) -> o d", o=1))
 
-        w2_raw = keep.tile([P, PASSES * PACK, HIDDEN], BF16)
+        w2_raw = keep.tile([P, FEATURE_TILES, HIDDEN], BF16)
         w3_raw = keep.tile([P, MODEL // P, HIDDEN], BF16)
         h1_raw = {}
         x1_raw = {}
 
-        def load_w2(g2):
+        def load_w2(g):
             nc.sync.dma_start(
-                out=w2_raw[:, g2 * PACK : (g2 + 1) * PACK, :].rearrange("m (a e) k -> m a (e k)", e=2),
-                in_=ffn_w2[g2 * CHUNK : (g2 + 1) * CHUNK, :].rearrange("(a m e) k -> m a (e k)", m=P, e=2),
+                out=w2_raw[:, g * PACK : (g + 1) * PACK, :].rearrange("m (u e) k -> m u (e k)", e=2),
+                in_=ffn_w2[g * P * PACK : (g + 1) * P * PACK, :].rearrange(
+                    "(u m e) k -> m u (e k)", m=P, e=2
+                ),
             )
 
         def load_h1(c):
@@ -207,11 +210,11 @@ def tile_transreachencoderlayer_pb_t_kernel(
 
         b2_bank = banks.tile([P, 2, 2 * P], F32, tag="bank")
         nc.tensor.transpose(out=b2_bank[:, 0, 0:P], in_=b2_rows[:].bitcast(F32), identity=identity[:])
-        b2_words = keep.tile([P, PASSES * PACK // 2], F32)
-        nc.vector.tensor_copy(out=b2_words[:], in_=b2_bank[:, 0, 0 : PASSES * PACK // 2])
-        b2_cols = keep.tile([P, PASSES * PACK], F32)
+        b2_words = keep.tile([P, FEATURE_TILES // 2], F32)
+        nc.vector.tensor_copy(out=b2_words[:], in_=b2_bank[:, 0, 0 : FEATURE_TILES // 2])
+        b2_cols = keep.tile([P, FEATURE_TILES], F32)
         nc.vector.tensor_copy(out=b2_cols[:], in_=b2_words[:].bitcast(BF16))
-        turn_bias = keep.tile([P, PASSES * PACK], F32)
+        turn_bias = keep.tile([P, FEATURE_TILES], F32)
         nc.vector.tensor_scalar(
             out=turn_bias[:], in0=b2_cols[:], scalar1=1.0 / TWO_PI, scalar2=phase_turns[:, 0:1],
             op0=ALU.mult, op1=ALU.add,
@@ -227,44 +230,41 @@ def tile_transreachencoderlayer_pb_t_kernel(
                 grouped = k_onto_partitions(
                     nc, banks, stage, tag, identity[:], nc.vector.tensor_copy, rows, n_tiles, g
                 )
-                quantise(nc, grouped, g, codes, scales)
+                quantise(nc, grouped[:], g, codes, scales)
 
-        h1_codes = {}
-        h1_scales = {}
-
-        h1_grouped = {}
-
-        def group_h1(q):
-            c, g = divmod(q, PASSES)
-            h1_grouped[q] = k_onto_partitions(
-                nc, banks, stage, "h1_grouped", identity[:], nc.scalar.copy, h1_raw[c][:], ROW_TILES, g
-            )
-
-        def quantise_h1(q):
-            c, g = divmod(q, PASSES)
-            if g == 0:
-                h1_codes[c] = stage.tile([P, PASSES, CHUNK], U32, tag="h1_codes", name="h1_codes", align_bytes=64)
-                h1_scales[c] = stage.tile([P, PASSES, CHUNK], U8, tag="h1_scales", name="h1_scales", align_bytes=64)
-            quantise(nc, h1_grouped[q], g, h1_codes[c], h1_scales[c])
-
-        def w2_half(g2):
-            cols = slice(g2 * CHUNK, (g2 + 1) * CHUNK)
+        def prepare_w2(g2):
+            cols = slice(g2 * PACK * P, (g2 + 1) * PACK * P)
             prepare_weight(
                 w2_raw[:, g2 * PACK : (g2 + 1) * PACK, :], PACK, "w2_grouped",
                 w2_codes[:, :, cols], w2_scales[:, :, cols],
             )
 
-
-        turns_of = {}
-        whole_of = {}
+        h1_grouped = {}
+        h1_codes = {}
+        h1_scales = {}
+        turns = {}
+        whole = {}
         h2_grouped = {}
         h2_codes = {}
         h2_scales = {}
         residual = {}
 
-        def first_matmul(i):
-            c, g2 = divmod(i, PASSES)
-            turns_of[i] = wave.tile([P, PACK, CHUNK], F32, tag="turns", name="turns")
+        def group_h1(unit):
+            c, g = divmod(unit, PASSES)
+            h1_grouped[unit] = k_onto_partitions(
+                nc, banks, stage, "h1_grouped", identity[:], nc.scalar.copy, h1_raw[c][:], ROW_TILES, g
+            )
+
+        def quantise_h1(unit):
+            c, g = divmod(unit, PASSES)
+            if g == 0:
+                h1_codes[c] = stage.tile([P, PASSES, CHUNK], U32, tag="h1_codes", name="h1_codes", align_bytes=64)
+                h1_scales[c] = stage.tile([P, PASSES, CHUNK], U8, tag="h1_scales", name="h1_scales", align_bytes=64)
+            quantise(nc, h1_grouped[unit][:], g, h1_codes[c], h1_scales[c])
+
+        def first_matmul(unit):
+            c, g2 = divmod(unit, PASSES)
+            turns[unit] = wave.tile([P, PACK, CHUNK], F32, tag="turns", name="turns")
             for t in range(PACK):
                 j = g2 * PACK + t
                 acc = u2_banks.tile([P, CHUNK], F32, tag="u2")
@@ -279,45 +279,43 @@ def tile_transreachencoderlayer_pb_t_kernel(
                         stop=(g == PASSES - 1),
                     )
                 nc.scalar.activation(
-                    out=turns_of[i][:, t, :], in_=acc[:], func=ACT.Identity,
+                    out=turns[unit][:, t, :], in_=acc[:], func=ACT.Identity,
                     bias=turn_bias[:, j : j + 1], scale=1.0 / TWO_PI,
                 )
 
-        def nearest_whole_turns(i):
-            whole_of[i] = wave.tile([P, PACK, CHUNK], F32, tag="whole", name="whole", bufs=2)
+        def nearest_whole_turns(unit):
+            whole[unit] = wave.tile([P, PACK, CHUNK], F32, tag="whole", name="whole")
             nc.vector.tensor_scalar(
-                out=whole_of[i][:], in0=turns_of[i][:], scalar1=ROUND_MAGIC, scalar2=ROUND_MAGIC,
+                out=whole[unit][:], in0=turns[unit][:], scalar1=ROUND_MAGIC, scalar2=ROUND_MAGIC,
                 op0=ALU.add, op1=ALU.subtract,
             )
 
-        def drop_whole_turns(i):
+        def drop_whole_turns(unit):
             nc.vector.tensor_tensor(
-                out=turns_of[i][:], in0=turns_of[i][:], in1=whole_of[i][:], op=ALU.subtract
+                out=turns[unit][:], in0=turns[unit][:], in1=whole[unit][:], op=ALU.subtract
             )
 
-        def sine(i):
-            nc.scalar.activation(out=turns_of[i][:], in_=turns_of[i][:], func=ACT.Sin, scale=TWO_PI)
+        def sine(unit):
+            nc.scalar.activation(out=turns[unit][:], in_=turns[unit][:], func=ACT.Sin, scale=TWO_PI)
 
-        def gain(i):
-            h2_grouped[i] = stage.tile([P, CHUNK, PACK], BF16, tag="h2_grouped", name="h2_grouped", align_bytes=64)
+        def gain(unit):
+            h2_grouped[unit] = stage.tile([P, CHUNK, PACK], BF16, tag="h2_grouped", name="h2_grouped", align_bytes=64)
             nc.vector.tensor_scalar(
-                out=h2_grouped[i][:], in0=turns_of[i][:].rearrange("p t n -> p n t"),
+                out=h2_grouped[unit][:].rearrange("p (n i) t -> p n t i", i=4),
+                in0=turns[unit][:].rearrange("p t (n i) -> p n t i", i=4),
                 scalar1=amp[:, 0:1], scalar2=None, op0=ALU.mult,
             )
 
-        def quantise_h2(i):
-            c, g2 = divmod(i, PASSES)
+        def quantise_h2(unit):
+            c, g2 = divmod(unit, PASSES)
             if g2 == 0:
                 h2_codes[c] = stage.tile([P, PASSES, CHUNK], U32, tag="h2_codes", name="h2_codes", align_bytes=64)
                 h2_scales[c] = stage.tile([P, PASSES, CHUNK], U8, tag="h2_scales", name="h2_scales", align_bytes=64)
-            nc.vector.quantize_mx(
-                out=h2_codes[c][:, g2, :].bitcast(FP8X4), scales=h2_scales[c][:, g2, :],
-                in_=h2_grouped[i][:].rearrange("p n t -> p (n t)"),
-            )
+            quantise(nc, h2_grouped[unit][:].rearrange("p n t -> p (n t)"), g2, h2_codes[c], h2_scales[c])
 
-        def residual_and_bias(r):
-            c, first = r // 2, 2 * (r % 2)
-            residual[r] = loads.tile([P, 2, MODEL], F32, tag="residual", name="residual", bufs=5)
+        def residual_and_bias(unit):
+            c, first = unit // 2, 2 * (unit % 2)
+            residual[unit] = loads.tile([P, 2, MODEL], F32, tag="residual", name="residual", bufs=SECOND_LAG + 1)
             bank = banks.tile([P, 2, MODEL], F32, tag="bank")
             for i in range(2):
                 nc.tensor.matmul(
@@ -327,10 +325,10 @@ def tile_transreachencoderlayer_pb_t_kernel(
                 nc.tensor.matmul(
                     out=bank[:, i, :], lhsT=first_row[:], rhs=b3_row[:], start=False, stop=True
                 )
-            nc.scalar.copy(out=residual[r][:], in_=bank[:])
+            nc.scalar.copy(out=residual[unit][:], in_=bank[:])
 
-        def second_matmul(r):
-            c, first = r // 2, 2 * (r % 2)
+        def second_matmul(unit):
+            c, first = unit // 2, 2 * (unit % 2)
             acc2 = out_banks.tile([P, 2, MODEL], F32, tag="acc2")
             for i in range(2):
                 tok = slice((first + i) * P, (first + i + 1) * P)
@@ -345,46 +343,49 @@ def tile_transreachencoderlayer_pb_t_kernel(
                         stop=(g2 == PASSES - 1),
                     )
             result = loads.tile([P, 2, MODEL], F32, tag="result")
-            nc.vector.tensor_tensor(out=result[:], in0=acc2[:], in1=residual[r][:], op=ALU.add)
+            nc.vector.tensor_tensor(out=result[:], in0=acc2[:], in1=residual[unit][:], op=ALU.add)
             nc.sync.dma_start(out=out_chunks[c][:, first : first + 2, :], in_=result[:])
 
-        w2_half(0)
+        prepare_w2(0)
         group_h1(0)
         group_h1(1)
         load_h1(3)
         quantise_h1(0)
         quantise_h1(1)
         first_matmul(0)
-        w2_half(1)
+        prepare_w2(1)
         group_h1(2)
         group_h1(3)
         quantise_h1(2)
         prepare_weight(w3_raw[:], MODEL // P, "w3_grouped", w3_codes[:], w3_scales[:])
 
+        def due(unit):
+            return 0 <= unit < UNITS
+
         with tc.manual_schedule():
-            for i in range(N_HALVES + 3):
-                if 1 <= i <= N_HALVES:
-                    sine(i - 1)
-                if 2 <= i <= N_HALVES + 1:
-                    quantise_h2(i - 2)
-                if i + 3 < N_HALVES:
-                    quantise_h1(i + 3)
-                if i + 1 < N_HALVES:
-                    first_matmul(i + 1)
-                if i < N_HALVES:
-                    nearest_whole_turns(i)
-                if i + 4 < N_HALVES:
-                    group_h1(i + 4)
-                if i < N_HALVES:
-                    residual_and_bias(i)
-                if i >= 3:
-                    second_matmul(i - 3)
-                if 1 <= i <= N_HALVES:
-                    gain(i - 1)
-                if i < N_HALVES:
-                    drop_whole_turns(i)
-                if i % 2 == 0:
-                    if i // 2 + 4 < N_CHUNKS:
-                        load_h1(i // 2 + 4)
-                    if i // 2 + 1 < N_CHUNKS:
-                        load_x1(i // 2 + 1)
+            for step in range(UNITS + SECOND_LAG):
+                if due(step - 1):
+                    sine(step - 1)
+                if due(step + 1):
+                    first_matmul(step + 1)
+                if due(step):
+                    nearest_whole_turns(step)
+                if due(step + 3):
+                    quantise_h1(step + 3)
+                if due(step):
+                    drop_whole_turns(step)
+                if due(step + 4):
+                    group_h1(step + 4)
+                if due(step):
+                    residual_and_bias(step)
+                if due(step - 1):
+                    gain(step - 1)
+                if due(step - 2):
+                    quantise_h2(step - 2)
+                if due(step - SECOND_LAG):
+                    second_matmul(step - SECOND_LAG)
+                if step % 2 == 0:
+                    if step // 2 + 4 < N_CHUNKS:
+                        load_h1(step // 2 + 4)
+                    if step // 2 + 1 < N_CHUNKS:
+                        load_x1(step // 2 + 1)

@@ -7,6 +7,7 @@ from concourse.masks import make_identity
 F32 = mybir.dt.float32
 BF16 = mybir.dt.bfloat16
 U32 = mybir.dt.uint32
+I32 = mybir.dt.int32
 U8 = mybir.dt.uint8
 FP8X4 = mybir.dt.float8_e4m3fn_x4
 ALU = mybir.AluOpType
@@ -31,116 +32,10 @@ TINY = 1e-30
 SECOND_LAG = 4
 PHASE_STEPS = 3
 
+SPARE_BANKS_FROM_END = 4
+GAIN_ON_SCALAR = ()
+
 FLOPS = 2 * TOKENS * HIDDEN * HIDDEN + 2 * TOKENS * HIDDEN * MODEL
-
-
-def k_onto_partitions(nc, banks, stage, tag, identity, copy, rows, n_tiles, g):
-    words = rows.bitcast(F32)
-    grouped = stage.tile([P, n_tiles * P * PACK], BF16, tag=tag, align_bytes=64)
-    pairs = grouped[:].bitcast(F32).rearrange("p (r u) -> p r u", u=2)
-    for first in range(0, n_tiles, 2):
-        bank = banks.tile([P, 2, 2 * P], F32, tag="bank")
-        for u in range(2):
-            for i in range(2):
-                w0 = g * WORDS + u * P
-                nc.tensor.transpose(
-                    out=bank[:, u, i * P : (i + 1) * P],
-                    in_=words[:, first + i, w0 : w0 + P],
-                    identity=identity,
-                )
-        copy(out=pairs[:, first * P : (first + 2) * P, :], in_=bank[:].rearrange("p u r -> p r u"))
-    return grouped
-
-
-def quantise(nc, grouped, g, codes, scales):
-    nc.vector.quantize_mx(out=codes[:, g, :].bitcast(FP8X4), scales=scales[:, g, :], in_=grouped)
-
-
-def wave_constants(nc, keep, w1_dram, w2_dram):
-    warm = keep.tile([P, 1], F32)
-    nc.vector.memset(warm[:], 0.0)
-    nc.scalar.activation(out=warm[:], in_=warm[:], func=ACT.Sin)
-
-    w1_bf = keep.tile([P, 1], BF16)
-    w2_bf = keep.tile([P, 1], BF16)
-    nc.sync.dma_start(out=w1_bf[:], in_=w1_dram.partition_broadcast(P))
-    nc.sync.dma_start(out=w2_bf[:], in_=w2_dram.partition_broadcast(P))
-    gains = keep.tile([P, 2], F32)
-    nc.vector.tensor_copy(out=gains[:, 0:1], in_=w1_bf[:])
-    nc.vector.tensor_copy(out=gains[:, 1:2], in_=w2_bf[:])
-
-    minus_half = keep.tile([P, 1], F32)
-    w1_sq = keep.tile([P, 1], F32)
-    amp_sq = keep.tile([P, 1], F32)
-    inv_amp = keep.tile([P, 1], F32)
-    nc.vector.memset(minus_half[:], -0.5)
-    nc.vector.tensor_scalar(
-        out=w1_sq[:], in0=gains[:, 0:1], scalar1=gains[:, 0:1], scalar2=TINY,
-        op0=ALU.mult, op1=ALU.add,
-    )
-    nc.vector.tensor_scalar(
-        out=amp_sq[:], in0=gains[:, 1:2], scalar1=gains[:, 1:2], scalar2=w1_sq[:, 0:1],
-        op0=ALU.mult, op1=ALU.add,
-    )
-    nc.gpsimd.tensor_tensor(out=inv_amp[:], in0=amp_sq[:], in1=minus_half[:], op=ALU.pow)
-
-    half = keep.tile([P, 1], F32)
-    coef = keep.tile([P, 1], F32)
-    ab = keep.tile([P, 2], F32)
-    nc.vector.tensor_scalar(
-        out=half[:], in0=gains[:, 1:2], scalar1=0.0, scalar2=0.5, op0=ALU.is_ge, op1=ALU.subtract
-    )
-    nc.vector.tensor_scalar(
-        out=coef[:], in0=half[:], scalar1=-2.0, scalar2=inv_amp[:, 0:1], op0=ALU.mult, op1=ALU.mult
-    )
-    nc.vector.tensor_scalar(out=ab[:], in0=gains[:], scalar1=coef[:, 0:1], scalar2=None, op0=ALU.mult)
-
-    angles = keep.tile([P, 2], F32)
-    cos_sin = keep.tile([P, 2], F32)
-    partial = keep.tile([P, 1], F32)
-    psi = angles[:, 1:2]
-    nc.vector.tensor_copy(out=psi, in_=ab[:, 0:1])
-
-    def cos_and_sin_of_psi():
-        nc.vector.tensor_scalar(
-            out=angles[:, 0:1], in0=psi, scalar1=0.5 * math.pi, scalar2=None, op0=ALU.add
-        )
-        nc.scalar.activation(out=cos_sin[:], in_=angles[:], func=ACT.Sin)
-
-    for repeat in range(PHASE_STEPS):
-        cos_and_sin_of_psi()
-        nc.vector.tensor_scalar(
-            out=partial[:], in0=cos_sin[:, 0:1], scalar1=ab[:, 0:1], scalar2=psi,
-            op0=ALU.mult, op1=ALU.add,
-        )
-        nc.vector.tensor_scalar(
-            out=psi, in0=cos_sin[:, 1:2], scalar1=ab[:, 1:2], scalar2=partial[:, 0:1],
-            op0=ALU.mult, op1=ALU.add,
-        )
-
-    quarter_turn = keep.tile([P, 1], F32)
-    phase_turns = keep.tile([P, 1], F32)
-    nc.vector.tensor_scalar(out=quarter_turn[:], in0=half[:], scalar1=0.5, scalar2=None, op0=ALU.mult)
-    nc.vector.tensor_scalar(
-        out=phase_turns[:], in0=psi, scalar1=1.0 / TWO_PI, scalar2=quarter_turn[:, 0:1],
-        op0=ALU.mult, op1=ALU.add,
-    )
-
-    signed = keep.tile([P, 2], F32)
-    w1_part = keep.tile([P, 1], F32)
-    amp = keep.tile([P, 1], F32)
-    nc.vector.tensor_scalar(
-        out=signed[:], in0=gains[:], scalar1=half[:, 0:1], scalar2=2.0, op0=ALU.mult, op1=ALU.mult
-    )
-    cos_and_sin_of_psi()
-    nc.vector.tensor_scalar(
-        out=w1_part[:], in0=cos_sin[:, 1:2], scalar1=signed[:, 0:1], scalar2=None, op0=ALU.mult
-    )
-    nc.vector.tensor_scalar(
-        out=amp[:], in0=cos_sin[:, 0:1], scalar1=signed[:, 1:2], scalar2=w1_part[:, 0:1],
-        op0=ALU.mult, op1=ALU.subtract,
-    )
-    return amp, phase_turns
 
 
 def tile_transreachencoderlayer_pb_t_kernel(
@@ -159,89 +54,190 @@ def tile_transreachencoderlayer_pb_t_kernel(
         banks = pools.enter_context(tc.psum_pool(name="banks", bufs=3))
         u2_banks = pools.enter_context(tc.psum_pool(name="u2_banks", bufs=PACK))
         out_banks = pools.enter_context(tc.psum_pool(name="out_banks", bufs=1))
+        pools.enter_context(tc.manual_schedule())
 
-        amp, phase_turns = wave_constants(nc, keep, ffn_a2w1, ffn_a2w2)
+        warm = keep.tile([P, 1], F32)
+        w1_bf = keep.tile([P, 1], BF16)
+        w2_bf = keep.tile([P, 1], BF16)
+        minus_half = keep.tile([P, 1], F32)
         b2_rows = keep.tile([P, 2 * P], BF16)
-        nc.vector.memset(b2_rows[:], 0.0)
-        nc.sync.dma_start(
-            out=b2_rows[0 : FEATURE_TILES // 2, :],
-            in_=ffn_b2.rearrange("(a w) -> a w", a=FEATURE_TILES // 2),
-        )
         b3_row = keep.tile([P, MODEL], BF16)
-        nc.vector.memset(b3_row[:], 0.0)
-        nc.sync.dma_start(out=b3_row[0:1, :], in_=ffn_b3.rearrange("(o d) -> o d", o=1))
-
+        first_row = keep.tile([P, P], BF16)
+        identity = keep.tile([P, P], F32)
+        identity_bf = keep.tile([P, P], BF16)
         w2_raw = keep.tile([P, FEATURE_TILES, HIDDEN], BF16)
         w3_raw = keep.tile([P, MODEL // P, HIDDEN], BF16)
+        w2_codes = keep.tile([P, FEATURE_TILES, PASSES * P], U32, align_bytes=64)
+        w2_scales = keep.tile([P, FEATURE_TILES, PASSES * P], U8, align_bytes=64)
+        w3_codes = keep.tile([P, PASSES, MODEL], U32, align_bytes=64)
+        w3_scales = keep.tile([P, PASSES, MODEL], U8, align_bytes=64)
         h1_raw = {}
         x1_raw = {}
 
-        def load_w2(g):
+        nc.vector.memset(warm[:], 0.0)
+        nc.scalar.activation(out=warm[:], in_=warm[:], func=ACT.Sin)
+        nc.vector.memset(b2_rows[:], 0.0)
+        make_identity(nc, identity[:])
+        make_identity(nc, identity_bf[:])
+
+        def load_w2(g, u):
+            j = g * PACK + 2 * u
+            r0 = (g * PACK + 2 * u) * P
             nc.sync.dma_start(
-                out=w2_raw[:, g * PACK : (g + 1) * PACK, :].rearrange("m (u e) k -> m u (e k)", e=2),
-                in_=ffn_w2[g * P * PACK : (g + 1) * P * PACK, :].rearrange(
-                    "(u m e) k -> m u (e k)", m=P, e=2
-                ),
+                out=w2_raw[:, j : j + 2, :].rearrange("m e k -> m (e k)"),
+                in_=ffn_w2[r0 : r0 + 2 * P, :].rearrange("(m e) k -> m (e k)", e=2),
             )
 
-        def load_h1(c):
+        def load_h1(c, pieces):
             h1_raw[c] = loads.tile([P, ROW_TILES, HIDDEN], BF16, tag="h1_raw", name="h1_raw")
-            nc.sync.dma_start(out=h1_raw[c][:], in_=h1_chunks[c])
+            n = ROW_TILES // pieces
+            for piece in range(pieces):
+                rows = slice(piece * n, (piece + 1) * n)
+                nc.sync.dma_start(out=h1_raw[c][:, rows, :], in_=h1_chunks[c][:, rows, :])
 
         def load_x1(c):
             x1_raw[c] = loads.tile([P, ROW_TILES, MODEL], BF16, tag="x1_raw", name="x1_raw")
             nc.sync.dma_start(out=x1_raw[c][:], in_=x1_chunks[c])
 
-        load_w2(0)
-        load_h1(0)
-        load_w2(1)
-        load_h1(1)
-        load_x1(0)
-        nc.sync.dma_start(out=w3_raw[:], in_=ffn_w3.rearrange("(i p) k -> p i k", p=P))
-        load_h1(2)
-
-        identity = keep.tile([P, P], F32)
-        make_identity(nc, identity[:])
-        identity_bf = keep.tile([P, P], BF16)
-        make_identity(nc, identity_bf[:])
-        first_row = keep.tile([P, P], BF16)
+        nc.sync.dma_start(out=w1_bf[:], in_=ffn_a2w1.partition_broadcast(P))
+        nc.sync.dma_start(out=w2_bf[:], in_=ffn_a2w2.partition_broadcast(P))
+        nc.sync.dma_start(
+            out=b2_rows[0 : FEATURE_TILES // 2, :],
+            in_=ffn_b2.rearrange("(a w) -> a w", a=FEATURE_TILES // 2),
+        )
+        load_h1(0, 2)
+        load_w2(0, 0)
+        load_w2(0, 1)
+        load_w2(1, 0)
+        load_w2(1, 1)
+        load_h1(1, 1)
+        nc.vector.memset(minus_half[:], -0.5)
+        nc.vector.memset(b3_row[:], 0.0)
         nc.vector.memset(first_row[:], 0.0)
         nc.vector.memset(first_row[0:1, :], 1.0)
+        nc.sync.dma_start(out=b3_row[0:1, :], in_=ffn_b3.rearrange("(o d) -> o d", o=1))
+        load_x1(0)
+        nc.sync.dma_start(out=w3_raw[:], in_=ffn_w3.rearrange("(i p) k -> p i k", p=P))
+        load_h1(2, 1)
 
-        b2_bank = banks.tile([P, 2, 2 * P], F32, tag="bank")
-        nc.tensor.transpose(out=b2_bank[:, 0, 0:P], in_=b2_rows[:].bitcast(F32), identity=identity[:])
-        b2_words = keep.tile([P, FEATURE_TILES // 2], F32)
-        nc.vector.tensor_copy(out=b2_words[:], in_=b2_bank[:, 0, 0 : FEATURE_TILES // 2])
-        b2_cols = keep.tile([P, FEATURE_TILES], F32)
-        nc.vector.tensor_copy(out=b2_cols[:], in_=b2_words[:].bitcast(BF16))
-        turn_bias = keep.tile([P, FEATURE_TILES], F32)
-        nc.vector.tensor_scalar(
-            out=turn_bias[:], in0=b2_cols[:], scalar1=1.0 / TWO_PI, scalar2=phase_turns[:, 0:1],
-            op0=ALU.mult, op1=ALU.add,
+        gains = keep.tile([P, 2], F32)
+        w1_sq = keep.tile([P, 1], F32)
+        amp_sq = keep.tile([P, 1], F32)
+        inv_amp = keep.tile([P, 1], F32)
+        half = keep.tile([P, 1], F32)
+        coef = keep.tile([P, 1], F32)
+        ab = keep.tile([P, 2], F32)
+        angles = keep.tile([P, 2], F32)
+        cos_sin = keep.tile([P, 2], F32)
+        partial = keep.tile([P, 1], F32)
+        quarter_turn = keep.tile([P, 1], F32)
+        phase_turns = keep.tile([P, 1], F32)
+        signed = keep.tile([P, 2], F32)
+        w1_part = keep.tile([P, 1], F32)
+        amp = keep.tile([P, 1], F32)
+        psi = angles[:, 1:2]
+        ts = nc.vector.tensor_scalar
+
+        small = [
+            lambda: nc.vector.tensor_copy(out=gains[:, 0:1], in_=w1_bf[:]),
+            lambda: nc.vector.tensor_copy(out=gains[:, 1:2], in_=w2_bf[:]),
+            lambda: ts(out=w1_sq[:], in0=gains[:, 0:1], scalar1=gains[:, 0:1], scalar2=TINY, op0=ALU.mult, op1=ALU.add),
+            lambda: ts(out=half[:], in0=gains[:, 1:2], scalar1=0.0, scalar2=0.5, op0=ALU.is_ge, op1=ALU.subtract),
+            lambda: ts(out=amp_sq[:], in0=gains[:, 1:2], scalar1=gains[:, 1:2], scalar2=w1_sq[:, 0:1], op0=ALU.mult, op1=ALU.add),
+            lambda: nc.gpsimd.tensor_tensor(out=inv_amp[:], in0=amp_sq[:], in1=minus_half[:], op=ALU.pow),
+            lambda: ts(out=quarter_turn[:], in0=half[:], scalar1=0.5, scalar2=None, op0=ALU.mult),
+            lambda: ts(out=signed[:], in0=gains[:], scalar1=half[:, 0:1], scalar2=2.0, op0=ALU.mult, op1=ALU.mult),
+            lambda: ts(out=coef[:], in0=half[:], scalar1=-2.0, scalar2=inv_amp[:, 0:1], op0=ALU.mult, op1=ALU.mult),
+            lambda: ts(out=ab[:], in0=gains[:], scalar1=coef[:, 0:1], scalar2=None, op0=ALU.mult),
+            lambda: nc.vector.tensor_copy(out=psi, in_=ab[:, 0:1]),
+        ]
+        cos_and_sin_of_psi = [
+            lambda: ts(out=angles[:, 0:1], in0=psi, scalar1=0.5 * math.pi, scalar2=None, op0=ALU.add),
+            lambda: nc.scalar.activation(out=cos_sin[:], in_=angles[:], func=ACT.Sin),
+        ]
+        for repeat in range(PHASE_STEPS):
+            small.extend(cos_and_sin_of_psi)
+            small.extend([
+                lambda: ts(out=partial[:], in0=cos_sin[:, 0:1], scalar1=ab[:, 0:1], scalar2=psi, op0=ALU.mult, op1=ALU.add),
+                lambda: ts(out=psi, in0=cos_sin[:, 1:2], scalar1=ab[:, 1:2], scalar2=partial[:, 0:1], op0=ALU.mult, op1=ALU.add),
+            ])
+        small.append(
+            lambda: ts(out=phase_turns[:], in0=psi, scalar1=1.0 / TWO_PI, scalar2=quarter_turn[:, 0:1], op0=ALU.mult, op1=ALU.add)
         )
+        small.extend(cos_and_sin_of_psi)
+        small.extend([
+            lambda: ts(out=w1_part[:], in0=cos_sin[:, 1:2], scalar1=signed[:, 0:1], scalar2=None, op0=ALU.mult),
+            lambda: ts(out=amp[:], in0=cos_sin[:, 0:1], scalar1=signed[:, 1:2], scalar2=w1_part[:, 0:1], op0=ALU.mult, op1=ALU.subtract),
+        ])
+        dealt = [0]
 
-        w2_codes = keep.tile([P, PASSES, HIDDEN], U32, align_bytes=64)
-        w2_scales = keep.tile([P, PASSES, HIDDEN], U8, align_bytes=64)
-        w3_codes = keep.tile([P, PASSES, MODEL], U32, align_bytes=64)
-        w3_scales = keep.tile([P, PASSES, MODEL], U8, align_bytes=64)
+        def deal(count):
+            for repeat in range(count):
+                if dealt[0] < len(small):
+                    small[dealt[0]]()
+                    dealt[0] += 1
 
-        def prepare_weight(rows, n_tiles, tag, codes, scales):
+        def turn_rows(rows, first, g):
+            words = rows.bitcast(F32)
+            bank = banks.tile([P, 2, 2 * P], F32, tag="bank", name="bank")
+            for u in range(2):
+                for i in range(2):
+                    w0 = g * WORDS + u * P
+                    nc.tensor.transpose(
+                        out=bank[:, u, i * P : (i + 1) * P], in_=words[:, first + i, w0 : w0 + P],
+                        identity=identity[:],
+                    )
+            return bank
+
+        def lay_rows(copy, grouped, first, bank):
+            pairs = grouped.bitcast(F32).rearrange("p (r u) -> p r u", u=2)
+            copy(out=pairs[:, first * P : (first + 2) * P, :], in_=bank[:].rearrange("p u r -> p r u"))
+
+        w2_bank = {}
+        w2_grouped = {}
+
+        def turn_w2(j):
+            words = w2_raw[:].bitcast(F32)
+            w2_bank[j] = banks.tile([P, PASSES, 2, P], F32, tag="bank", name="bank")
             for g in range(PASSES):
-                grouped = k_onto_partitions(
-                    nc, banks, stage, tag, identity[:], nc.vector.tensor_copy, rows, n_tiles, g
-                )
-                quantise(nc, grouped[:], g, codes, scales)
+                for u in range(2):
+                    w0 = g * WORDS + u * P
+                    nc.tensor.transpose(
+                        out=w2_bank[j][:, g, u, :], in_=words[:, j, w0 : w0 + P], identity=identity[:]
+                    )
 
-        def prepare_w2(g2):
-            cols = slice(g2 * PACK * P, (g2 + 1) * PACK * P)
-            prepare_weight(
-                w2_raw[:, g2 * PACK : (g2 + 1) * PACK, :], PACK, "w2_grouped",
-                w2_codes[:, :, cols], w2_scales[:, :, cols],
+        def lay_w2(copy, j):
+            w2_grouped[j] = stage.tile([P, PASSES * P * PACK], BF16, tag="w2_grouped", name="w2_grouped", align_bytes=64)
+            copy(
+                out=w2_grouped[j][:].bitcast(F32).rearrange("p (g r u) -> p g r u", g=PASSES, u=2),
+                in_=w2_bank[j][:].rearrange("p g u r -> p g r u"),
             )
 
+        def quantise_w2(j):
+            nc.vector.quantize_mx(
+                out=w2_codes[:, j, :].bitcast(FP8X4), scales=w2_scales[:, j, :], in_=w2_grouped[j][:]
+            )
+
+        w3_bank = {}
+        w3_grouped = {}
+
+        def turn_w3(g):
+            w3_bank[g] = turn_rows(w3_raw[:], 0, g)
+
+        def lay_w3(copy, g):
+            w3_grouped[g] = stage.tile([P, MODEL * PACK], BF16, tag="w3_grouped", name="w3_grouped", align_bytes=64)
+            lay_rows(copy, w3_grouped[g][:], 0, w3_bank[g])
+
+        def quantise_w3(g):
+            nc.vector.quantize_mx(
+                out=w3_codes[:, g, :].bitcast(FP8X4), scales=w3_scales[:, g, :], in_=w3_grouped[g][:]
+            )
+
+        h1_bank = {}
         h1_grouped = {}
         h1_codes = {}
         h1_scales = {}
+        acc = {}
         turns = {}
         whole = {}
         h2_grouped = {}
@@ -249,50 +245,70 @@ def tile_transreachencoderlayer_pb_t_kernel(
         h2_scales = {}
         residual = {}
 
-        def group_h1(unit):
+        def turn_h1(unit, first):
             c, g = divmod(unit, PASSES)
-            h1_grouped[unit] = k_onto_partitions(
-                nc, banks, stage, "h1_grouped", identity[:], nc.scalar.copy, h1_raw[c][:], ROW_TILES, g
-            )
+            h1_bank[(unit, first)] = turn_rows(h1_raw[c][:], first, g)
+
+        def lay_h1(copy, unit, first):
+            if unit not in h1_grouped:
+                h1_grouped[unit] = stage.tile([P, CHUNK * PACK], BF16, tag="h1_grouped", name="h1_grouped", align_bytes=64)
+            lay_rows(copy, h1_grouped[unit][:], first, h1_bank[(unit, first)])
+
+        def group_h1(unit):
+            for first in range(0, ROW_TILES, 2):
+                turn_h1(unit, first)
+                lay_h1(nc.scalar.copy, unit, first)
 
         def quantise_h1(unit):
             c, g = divmod(unit, PASSES)
             if g == 0:
                 h1_codes[c] = stage.tile([P, PASSES, CHUNK], U32, tag="h1_codes", name="h1_codes", align_bytes=64)
                 h1_scales[c] = stage.tile([P, PASSES, CHUNK], U8, tag="h1_scales", name="h1_scales", align_bytes=64)
-            quantise(nc, h1_grouped[unit][:], g, h1_codes[c], h1_scales[c])
+            nc.vector.quantize_mx(
+                out=h1_codes[c][:, g, :].bitcast(FP8X4), scales=h1_scales[c][:, g, :], in_=h1_grouped[unit][:]
+            )
 
-        def first_matmul(unit):
+        def matmul_bank(unit, t):
             c, g2 = divmod(unit, PASSES)
-            turns[unit] = wave.tile([P, PACK, CHUNK], F32, tag="turns", name="turns")
-            for t in range(PACK):
-                j = g2 * PACK + t
-                acc = u2_banks.tile([P, CHUNK], F32, tag="u2")
-                for g in range(PASSES):
-                    nc.tensor.matmul_mx(
-                        out=acc[:],
-                        lhsT=w2_codes[:, g, j * P : (j + 1) * P].bitcast(FP8X4),
-                        lhsT_scale=w2_scales[:, g, j * P : (j + 1) * P],
-                        rhs=h1_codes[c][:, g, :].bitcast(FP8X4),
-                        rhs_scale=h1_scales[c][:, g, :],
-                        start=(g == 0),
-                        stop=(g == PASSES - 1),
-                    )
-                nc.scalar.activation(
-                    out=turns[unit][:, t, :], in_=acc[:], func=ACT.Identity,
-                    bias=turn_bias[:, j : j + 1], scale=1.0 / TWO_PI,
+            j = g2 * PACK + t
+            acc[(unit, t)] = u2_banks.tile([P, CHUNK], F32, tag="u2", name="u2")
+            for g in range(PASSES):
+                nc.tensor.matmul_mx(
+                    out=acc[(unit, t)][:],
+                    lhsT=w2_codes[:, j, g * P : (g + 1) * P].bitcast(FP8X4),
+                    lhsT_scale=w2_scales[:, j, g * P : (g + 1) * P],
+                    rhs=h1_codes[c][:, g, :].bitcast(FP8X4),
+                    rhs_scale=h1_scales[c][:, g, :],
+                    start=(g == 0),
+                    stop=(g == PASSES - 1),
                 )
 
+        def turns_bank(unit, t):
+            j = (unit % PASSES) * PACK + t
+            if t == 0:
+                turns[unit] = wave.tile([P, PACK, CHUNK], F32, tag="turns", name="turns")
+            nc.scalar.activation(
+                out=turns[unit][:, t, :], in_=acc[(unit, t)][:], func=ACT.Identity,
+                bias=b2_turns[:, j : j + 1], scale=1.0 / TWO_PI,
+            )
+
+        def first_matmul(unit):
+            for t in range(PACK):
+                matmul_bank(unit, t)
+                turns_bank(unit, t)
+
         def nearest_whole_turns(unit):
-            whole[unit] = wave.tile([P, PACK, CHUNK], F32, tag="whole", name="whole")
+            whole[unit] = wave.tile([P, PACK, CHUNK], I32, tag="whole", name="whole")
             nc.vector.tensor_scalar(
-                out=whole[unit][:], in0=turns[unit][:], scalar1=ROUND_MAGIC, scalar2=ROUND_MAGIC,
-                op0=ALU.add, op1=ALU.subtract,
+                out=whole[unit][:], in0=turns[unit][:], scalar1=phase_turns[:, 0:1], scalar2=None, op0=ALU.add
             )
 
         def drop_whole_turns(unit):
-            nc.vector.tensor_tensor(
-                out=turns[unit][:], in0=turns[unit][:], in1=whole[unit][:], op=ALU.subtract
+            flat = "p t n -> p (t n)"
+            nc.vector.scalar_tensor_tensor(
+                out=turns[unit][:].rearrange(flat), in0=turns[unit][:].rearrange(flat),
+                scalar=phase_turns[:, 0:1], in1=whole[unit][:].rearrange(flat),
+                op0=ALU.add, op1=ALU.subtract,
             )
 
         def sine(unit):
@@ -300,23 +316,33 @@ def tile_transreachencoderlayer_pb_t_kernel(
 
         def gain(unit):
             h2_grouped[unit] = stage.tile([P, CHUNK, PACK], BF16, tag="h2_grouped", name="h2_grouped", align_bytes=64)
-            nc.vector.tensor_scalar(
-                out=h2_grouped[unit][:].rearrange("p (n i) t -> p n t i", i=4),
-                in0=turns[unit][:].rearrange("p t (n i) -> p n t i", i=4),
-                scalar1=amp[:, 0:1], scalar2=None, op0=ALU.mult,
-            )
+            if unit in GAIN_ON_SCALAR:
+                nc.scalar.activation(
+                    out=h2_grouped[unit][:].rearrange("p (n i) t -> p n t i", i=4),
+                    in_=turns[unit][:].rearrange("p t (n i) -> p n t i", i=4),
+                    func=ACT.Copy, scale=amp[:, 0:1],
+                )
+            else:
+                nc.vector.tensor_scalar(
+                    out=h2_grouped[unit][:].rearrange("p (n i) t -> p n t i", i=4),
+                    in0=turns[unit][:].rearrange("p t (n i) -> p n t i", i=4),
+                    scalar1=amp[:, 0:1], scalar2=None, op0=ALU.mult,
+                )
 
         def quantise_h2(unit):
             c, g2 = divmod(unit, PASSES)
             if g2 == 0:
                 h2_codes[c] = stage.tile([P, PASSES, CHUNK], U32, tag="h2_codes", name="h2_codes", align_bytes=64)
                 h2_scales[c] = stage.tile([P, PASSES, CHUNK], U8, tag="h2_scales", name="h2_scales", align_bytes=64)
-            quantise(nc, h2_grouped[unit][:].rearrange("p n t -> p (n t)"), g2, h2_codes[c], h2_scales[c])
+            nc.vector.quantize_mx(
+                out=h2_codes[c][:, g2, :].bitcast(FP8X4), scales=h2_scales[c][:, g2, :],
+                in_=h2_grouped[unit][:].rearrange("p n t -> p (n t)"),
+            )
 
         def residual_and_bias(unit):
             c, first = unit // 2, 2 * (unit % 2)
             residual[unit] = loads.tile([P, 2, MODEL], F32, tag="residual", name="residual", bufs=SECOND_LAG + 1)
-            bank = banks.tile([P, 2, MODEL], F32, tag="bank")
+            bank = banks.tile([P, 2, MODEL], F32, tag="bank", name="bank")
             for i in range(2):
                 nc.tensor.matmul(
                     out=bank[:, i, :], lhsT=identity_bf[:], rhs=x1_raw[c][:, first + i, :],
@@ -329,7 +355,10 @@ def tile_transreachencoderlayer_pb_t_kernel(
 
         def second_matmul(unit):
             c, first = unit // 2, 2 * (unit % 2)
-            acc2 = out_banks.tile([P, 2, MODEL], F32, tag="acc2")
+            if unit + SPARE_BANKS_FROM_END >= UNITS:
+                acc2 = banks.tile([P, 2, MODEL], F32, tag="bank", name="bank")
+            else:
+                acc2 = out_banks.tile([P, 2, MODEL], F32, tag="acc2", name="acc2")
             for i in range(2):
                 tok = slice((first + i) * P, (first + i + 1) * P)
                 for g2 in range(PASSES):
@@ -342,50 +371,133 @@ def tile_transreachencoderlayer_pb_t_kernel(
                         start=(g2 == 0),
                         stop=(g2 == PASSES - 1),
                     )
-            result = loads.tile([P, 2, MODEL], F32, tag="result")
+            result = loads.tile([P, 2, MODEL], F32, tag="result", name="result")
             nc.vector.tensor_tensor(out=result[:], in0=acc2[:], in1=residual[unit][:], op=ALU.add)
             nc.sync.dma_start(out=out_chunks[c][:, first : first + 2, :], in_=result[:])
 
-        prepare_w2(0)
-        group_h1(0)
-        group_h1(1)
-        load_h1(3)
+        b2_bank = banks.tile([P, 2, 2 * P], F32, tag="bank", name="bank")
+        b2_words = keep.tile([P, FEATURE_TILES // 2], F32)
+        b2_cols = keep.tile([P, FEATURE_TILES], F32)
+        b2_turns = keep.tile([P, FEATURE_TILES], F32)
+        by_scalar = nc.scalar.copy
+        by_vector = nc.vector.tensor_copy
+        deal(6)
+        nc.tensor.transpose(out=b2_bank[:, 0, 0:P], in_=b2_rows[:].bitcast(F32), identity=identity[:])
+        nc.vector.tensor_copy(out=b2_words[:], in_=b2_bank[:, 0, 0 : FEATURE_TILES // 2])
+        deal(1)
+        nc.vector.tensor_copy(out=b2_cols[:], in_=b2_words[:].bitcast(BF16))
+        deal(1)
+        nc.vector.tensor_scalar(out=b2_turns[:], in0=b2_cols[:], scalar1=1.0 / TWO_PI, scalar2=None, op0=ALU.mult)
+        deal(4)
+        turn_h1(0, 0)
+        turn_h1(1, 0)
+        lay_h1(by_scalar, 0, 0)
+        deal(1)
+        lay_h1(by_vector, 1, 0)
+        turn_h1(0, 2)
+        turn_h1(1, 2)
+        lay_h1(by_scalar, 0, 2)
+        deal(1)
+        lay_h1(by_vector, 1, 2)
+        load_h1(3, 1)
+        deal(1)
+        turn_w2(0)
+        turn_w2(1)
         quantise_h1(0)
+        lay_w2(by_scalar, 0)
+        deal(1)
+        turn_w2(2)
         quantise_h1(1)
-        first_matmul(0)
-        prepare_w2(1)
-        group_h1(2)
-        group_h1(3)
+        lay_w2(by_scalar, 1)
+        deal(1)
+        turn_w2(3)
+        quantise_w2(0)
+        lay_w2(by_scalar, 2)
+        deal(1)
+        turn_w2(4)
+        quantise_w2(1)
+        lay_w2(by_scalar, 3)
+        deal(1)
+        turn_w2(5)
+        quantise_w2(2)
+        deal(1)
+        matmul_bank(0, 0)
+        quantise_w2(3)
+        matmul_bank(0, 1)
+        lay_w2(by_vector, 4)
+        turns_bank(0, 0)
+        matmul_bank(0, 2)
+        lay_w2(by_vector, 5)
+        turns_bank(0, 1)
+        matmul_bank(0, 3)
+        deal(1)
+        quantise_w2(4)
+        turns_bank(0, 2)
+        deal(1)
+        quantise_w2(5)
+        turns_bank(0, 3)
+        turn_w2(6)
+        turn_w2(7)
+        turn_h1(2, 0)
+        deal(2)
+        lay_w2(by_scalar, 6)
+        turn_h1(2, 2)
+        lay_w2(by_scalar, 7)
+        turn_h1(3, 0)
+        nearest_whole_turns(0)
+        lay_h1(by_scalar, 2, 0)
+        turn_h1(3, 2)
+        quantise_w2(6)
+        deal(1)
+        quantise_w2(7)
+        deal(1)
+        lay_h1(by_scalar, 2, 2)
+        for t in range(PACK):
+            matmul_bank(1, t)
+        drop_whole_turns(0)
+        deal(1)
+        lay_h1(by_vector, 3, 0)
+        deal(1)
+        lay_h1(by_vector, 3, 2)
+        deal(len(small))
+        for t in range(PACK):
+            turns_bank(1, t)
         quantise_h1(2)
-        prepare_weight(w3_raw[:], MODEL // P, "w3_grouped", w3_codes[:], w3_scales[:])
 
         def due(unit):
             return 0 <= unit < UNITS
 
-        with tc.manual_schedule():
-            for step in range(UNITS + SECOND_LAG):
-                if due(step - 1):
-                    sine(step - 1)
-                if due(step + 1):
-                    first_matmul(step + 1)
-                if due(step):
-                    nearest_whole_turns(step)
-                if due(step + 3):
-                    quantise_h1(step + 3)
-                if due(step):
-                    drop_whole_turns(step)
-                if due(step + 4):
-                    group_h1(step + 4)
-                if due(step):
-                    residual_and_bias(step)
-                if due(step - 1):
-                    gain(step - 1)
-                if due(step - 2):
-                    quantise_h2(step - 2)
-                if due(step - SECOND_LAG):
-                    second_matmul(step - SECOND_LAG)
-                if step % 2 == 0:
-                    if step // 2 + 4 < N_CHUNKS:
-                        load_h1(step // 2 + 4)
-                    if step // 2 + 1 < N_CHUNKS:
-                        load_x1(step // 2 + 1)
+        for step in range(UNITS + SECOND_LAG):
+            if due(step - 1):
+                sine(step - 1)
+            if step == 1 or step == 2:
+                turn_w3(step - 1)
+            if due(step + 1) and step > 0:
+                first_matmul(step + 1)
+            if due(step) and step > 0:
+                nearest_whole_turns(step)
+            if due(step + 3):
+                quantise_h1(step + 3)
+            elif due(step - 2):
+                quantise_h2(step - 2)
+            if due(step) and step > 0:
+                drop_whole_turns(step)
+            if due(step + 4):
+                group_h1(step + 4)
+            if due(step):
+                residual_and_bias(step)
+            if due(step - 1):
+                gain(step - 1)
+            if step == 1 or step == 2:
+                lay_w3(nc.vector.tensor_copy, step - 1)
+            if due(step + 3) and due(step - 2):
+                quantise_h2(step - 2)
+            if step == 2 or step == 3:
+                quantise_w3(step - 2)
+            if due(step - SECOND_LAG):
+                second_matmul(step - SECOND_LAG)
+            if step % 2 == 0:
+                if step // 2 + 4 < N_CHUNKS:
+                    load_h1(step // 2 + 4, 1)
+                if step // 2 + 1 < N_CHUNKS:
+                    load_x1(step // 2 + 1)

@@ -32,8 +32,7 @@ TINY = 1e-30
 SECOND_LAG = 4
 PHASE_STEPS = 3
 
-SPARE_BANKS_FROM_END = 4
-GAIN_ON_SCALAR = ()
+SPARE_BANKS_FROM_END = 5
 
 FLOPS = 2 * TOKENS * HIDDEN * HIDDEN + 2 * TOKENS * HIDDEN * MODEL
 
@@ -297,46 +296,52 @@ def tile_transreachencoderlayer_pb_t_kernel(
                 matmul_bank(unit, t)
                 turns_bank(unit, t)
 
-        def nearest_whole_turns(unit):
-            whole[unit] = wave.tile([P, PACK, CHUNK], I32, tag="whole", name="whole")
+        ALL = slice(0, CHUNK)
+
+        def nearest_whole_turns(unit, tokens=ALL):
+            if unit not in whole:
+                whole[unit] = wave.tile([P, PACK, CHUNK], I32, tag="whole", name="whole")
             nc.vector.tensor_scalar(
-                out=whole[unit][:], in0=turns[unit][:], scalar1=phase_turns[:, 0:1], scalar2=None, op0=ALU.add
+                out=whole[unit][:, :, tokens], in0=turns[unit][:, :, tokens], scalar1=phase_turns[:, 0:1],
+                scalar2=None, op0=ALU.add,
             )
 
-        def drop_whole_turns(unit):
-            flat = "p t n -> p (t n)"
+        def drop_whole_turns(unit, tokens=ALL):
             nc.vector.scalar_tensor_tensor(
-                out=turns[unit][:].rearrange(flat), in0=turns[unit][:].rearrange(flat),
-                scalar=phase_turns[:, 0:1], in1=whole[unit][:].rearrange(flat),
+                out=turns[unit][:, :, tokens], in0=turns[unit][:, :, tokens],
+                scalar=phase_turns[:, 0:1], in1=whole[unit][:, :, tokens],
                 op0=ALU.add, op1=ALU.subtract,
             )
 
-        def sine(unit):
-            nc.scalar.activation(out=turns[unit][:], in_=turns[unit][:], func=ACT.Sin, scale=TWO_PI)
+        def sine(unit, tokens=ALL):
+            nc.scalar.activation(
+                out=turns[unit][:, :, tokens], in_=turns[unit][:, :, tokens], func=ACT.Sin, scale=TWO_PI
+            )
 
-        def gain(unit):
-            h2_grouped[unit] = stage.tile([P, CHUNK, PACK], BF16, tag="h2_grouped", name="h2_grouped", align_bytes=64)
-            if unit in GAIN_ON_SCALAR:
+        def gain(unit, tokens=ALL, on_scalar=False):
+            if unit not in h2_grouped:
+                h2_grouped[unit] = stage.tile([P, CHUNK, PACK], BF16, tag="h2_grouped", name="h2_grouped", align_bytes=64)
+            if on_scalar:
                 nc.scalar.activation(
-                    out=h2_grouped[unit][:].rearrange("p (n i) t -> p n t i", i=4),
-                    in_=turns[unit][:].rearrange("p t (n i) -> p n t i", i=4),
+                    out=h2_grouped[unit][:, tokens, :].rearrange("p (n i) t -> p n t i", i=4),
+                    in_=turns[unit][:, :, tokens].rearrange("p t (n i) -> p n t i", i=4),
                     func=ACT.Copy, scale=amp[:, 0:1],
                 )
             else:
                 nc.vector.tensor_scalar(
-                    out=h2_grouped[unit][:].rearrange("p (n i) t -> p n t i", i=4),
-                    in0=turns[unit][:].rearrange("p t (n i) -> p n t i", i=4),
+                    out=h2_grouped[unit][:, tokens, :].rearrange("p (n i) t -> p n t i", i=4),
+                    in0=turns[unit][:, :, tokens].rearrange("p t (n i) -> p n t i", i=4),
                     scalar1=amp[:, 0:1], scalar2=None, op0=ALU.mult,
                 )
 
-        def quantise_h2(unit):
+        def quantise_h2(unit, tokens=ALL):
             c, g2 = divmod(unit, PASSES)
-            if g2 == 0:
+            if c not in h2_codes:
                 h2_codes[c] = stage.tile([P, PASSES, CHUNK], U32, tag="h2_codes", name="h2_codes", align_bytes=64)
                 h2_scales[c] = stage.tile([P, PASSES, CHUNK], U8, tag="h2_scales", name="h2_scales", align_bytes=64)
             nc.vector.quantize_mx(
-                out=h2_codes[c][:, g2, :].bitcast(FP8X4), scales=h2_scales[c][:, g2, :],
-                in_=h2_grouped[unit][:].rearrange("p n t -> p (n t)"),
+                out=h2_codes[c][:, g2, tokens].bitcast(FP8X4), scales=h2_scales[c][:, g2, tokens],
+                in_=h2_grouped[unit][:, tokens, :].rearrange("p n t -> p (n t)"),
             )
 
         def residual_and_bias(unit):
@@ -353,12 +358,15 @@ def tile_transreachencoderlayer_pb_t_kernel(
                 )
             nc.scalar.copy(out=residual[unit][:], in_=bank[:])
 
-        def second_matmul(unit):
+        sums = {}
+
+        def second_sums(unit):
             c, first = unit // 2, 2 * (unit % 2)
             if unit + SPARE_BANKS_FROM_END >= UNITS:
                 acc2 = banks.tile([P, 2, MODEL], F32, tag="bank", name="bank")
             else:
                 acc2 = out_banks.tile([P, 2, MODEL], F32, tag="acc2", name="acc2")
+            sums[unit] = acc2
             for i in range(2):
                 tok = slice((first + i) * P, (first + i + 1) * P)
                 for g2 in range(PASSES):
@@ -371,9 +379,16 @@ def tile_transreachencoderlayer_pb_t_kernel(
                         start=(g2 == 0),
                         stop=(g2 == PASSES - 1),
                     )
+
+        def second_add(unit):
+            c, first = unit // 2, 2 * (unit % 2)
             result = loads.tile([P, 2, MODEL], F32, tag="result", name="result")
-            nc.vector.tensor_tensor(out=result[:], in0=acc2[:], in1=residual[unit][:], op=ALU.add)
+            nc.vector.tensor_tensor(out=result[:], in0=sums[unit][:], in1=residual[unit][:], op=ALU.add)
             nc.sync.dma_start(out=out_chunks[c][:, first : first + 2, :], in_=result[:])
+
+        def second_matmul(unit):
+            second_sums(unit)
+            second_add(unit)
 
         b2_bank = banks.tile([P, 2, 2 * P], F32, tag="bank", name="bank")
         b2_words = keep.tile([P, FEATURE_TILES // 2], F32)
@@ -467,7 +482,7 @@ def tile_transreachencoderlayer_pb_t_kernel(
         def due(unit):
             return 0 <= unit < UNITS
 
-        for step in range(UNITS + SECOND_LAG):
+        for step in range(UNITS - 1):
             if due(step - 1):
                 sine(step - 1)
             if step == 1 or step == 2:
@@ -501,3 +516,31 @@ def tile_transreachencoderlayer_pb_t_kernel(
                     load_h1(step // 2 + 4, 1)
                 if step // 2 + 1 < N_CHUNKS:
                     load_x1(step // 2 + 1)
+
+        FIRST = slice(0, CHUNK // 2)
+        LAST = slice(CHUNK // 2, CHUNK)
+        sine(14)
+        nearest_whole_turns(15, FIRST)
+        nearest_whole_turns(15, LAST)
+        drop_whole_turns(15, FIRST)
+        quantise_h2(13)
+        drop_whole_turns(15, LAST)
+        residual_and_bias(15)
+        gain(14, ALL, True)
+        sine(15, FIRST)
+        sine(15, LAST)
+        second_sums(11)
+        second_add(11)
+        second_sums(12)
+        second_sums(13)
+        quantise_h2(14)
+        second_add(12)
+        gain(15, FIRST)
+        gain(15, LAST, True)
+        second_add(13)
+        quantise_h2(15, FIRST)
+        second_sums(14)
+        quantise_h2(15, LAST)
+        second_add(14)
+        second_sums(15)
+        second_add(15)

@@ -34,6 +34,8 @@ PHASE_STEPS = 3
 
 SPARE_BANKS_FROM_END = 5
 
+WARM_UP = 6
+
 FLOPS = 2 * TOKENS * HIDDEN * HIDDEN + 2 * TOKENS * HIDDEN * MODEL
 
 
@@ -73,6 +75,15 @@ def tile_transreachencoderlayer_pb_t_kernel(
         h1_raw = {}
         x1_raw = {}
 
+        zeros = keep.tile([P, CHUNK], BF16)
+        nc.vector.memset(zeros[:], 0.0)
+
+        def keep_clock_up(count):
+            for repeat in range(count):
+                unread = u2_banks.tile([P, CHUNK], F32, tag="u2", name="u2")
+                nc.tensor.matmul(out=unread[:], lhsT=zeros[:, 0:P], rhs=zeros[:], start=True, stop=True)
+
+        keep_clock_up(WARM_UP)
         nc.vector.memset(warm[:], 0.0)
         nc.scalar.activation(out=warm[:], in_=warm[:], func=ACT.Sin)
         nc.vector.memset(b2_rows[:], 0.0)
@@ -406,11 +417,13 @@ def tile_transreachencoderlayer_pb_t_kernel(
         deal(4)
         turn_h1(0, 0)
         turn_h1(1, 0)
+        keep_clock_up(1)
         lay_h1(by_scalar, 0, 0)
         deal(1)
         lay_h1(by_vector, 1, 0)
         turn_h1(0, 2)
         turn_h1(1, 2)
+        keep_clock_up(1)
         lay_h1(by_scalar, 0, 2)
         deal(1)
         lay_h1(by_vector, 1, 2)
@@ -418,6 +431,7 @@ def tile_transreachencoderlayer_pb_t_kernel(
         deal(1)
         turn_w2(0)
         turn_w2(1)
+        keep_clock_up(1)
         quantise_h1(0)
         lay_w2(by_scalar, 0)
         deal(1)
@@ -426,6 +440,7 @@ def tile_transreachencoderlayer_pb_t_kernel(
         lay_w2(by_scalar, 1)
         deal(1)
         turn_w2(3)
+        keep_clock_up(1)
         quantise_w2(0)
         lay_w2(by_scalar, 2)
         deal(1)
@@ -434,6 +449,7 @@ def tile_transreachencoderlayer_pb_t_kernel(
         lay_w2(by_scalar, 3)
         deal(1)
         turn_w2(5)
+        keep_clock_up(1)
         quantise_w2(2)
         deal(1)
         matmul_bank(0, 0)

@@ -32,9 +32,9 @@ TINY = 1e-30
 SECOND_LAG = 4
 PHASE_STEPS = 3
 
-SPARE_BANKS_FROM_END = 5
-
+SPARE_BANKS_FROM_END = 0
 WARM_UP = 6
+VIA_SCALAR = 3
 
 FLOPS = 2 * TOKENS * HIDDEN * HIDDEN + 2 * TOKENS * HIDDEN * MODEL
 
@@ -145,6 +145,9 @@ def tile_transreachencoderlayer_pb_t_kernel(
         signed = keep.tile([P, 2], F32)
         w1_part = keep.tile([P, 1], F32)
         amp = keep.tile([P, 1], F32)
+        b2_turns = keep.tile([P, FEATURE_TILES], F32)
+        turn_bias = keep.tile([P, FEATURE_TILES], F32)
+        angle_bias = keep.tile([P, FEATURE_TILES], F32)
         psi = angles[:, 1:2]
         ts = nc.vector.tensor_scalar
 
@@ -174,6 +177,10 @@ def tile_transreachencoderlayer_pb_t_kernel(
         small.append(
             lambda: ts(out=phase_turns[:], in0=psi, scalar1=1.0 / TWO_PI, scalar2=quarter_turn[:, 0:1], op0=ALU.mult, op1=ALU.add)
         )
+        small.extend([
+            lambda: ts(out=turn_bias[:], in0=b2_turns[:], scalar1=phase_turns[:, 0:1], scalar2=None, op0=ALU.add),
+            lambda: ts(out=angle_bias[:], in0=turn_bias[:], scalar1=TWO_PI, scalar2=None, op0=ALU.mult),
+        ])
         small.extend(cos_and_sin_of_psi)
         small.extend([
             lambda: ts(out=w1_part[:], in0=cos_sin[:, 1:2], scalar1=signed[:, 0:1], scalar2=None, op0=ALU.mult),
@@ -293,57 +300,62 @@ def tile_transreachencoderlayer_pb_t_kernel(
                     stop=(g == PASSES - 1),
                 )
 
+        ALL = slice(0, CHUNK)
+        angle = {}
+        amp_now = {}
+
         def turns_bank(unit, t):
             j = (unit % PASSES) * PACK + t
             if t == 0:
-                turns[unit] = wave.tile([P, PACK, CHUNK], F32, tag="turns", name="turns")
+                turns[unit] = wave.tile([P, VIA_SCALAR, CHUNK], F32, tag="turns", name="turns", bufs=2)
             nc.scalar.activation(
                 out=turns[unit][:, t, :], in_=acc[(unit, t)][:], func=ACT.Identity,
                 bias=b2_turns[:, j : j + 1], scale=1.0 / TWO_PI,
             )
 
-        def first_matmul(unit):
-            for t in range(PACK):
-                matmul_bank(unit, t)
-                turns_bank(unit, t)
-
-        ALL = slice(0, CHUNK)
-
-        def nearest_whole_turns(unit, tokens=ALL):
+        def whole_of(unit):
             if unit not in whole:
-                whole[unit] = wave.tile([P, PACK, CHUNK], I32, tag="whole", name="whole")
+                whole[unit] = wave.tile([P, PACK, CHUNK], I32, tag="whole", name="whole", bufs=2)
+            return whole[unit]
+
+        def round_turns(unit):
             nc.vector.tensor_scalar(
-                out=whole[unit][:, :, tokens], in0=turns[unit][:, :, tokens], scalar1=phase_turns[:, 0:1],
+                out=whole_of(unit)[:, 0:VIA_SCALAR, :], in0=turns[unit][:], scalar1=phase_turns[:, 0:1],
                 scalar2=None, op0=ALU.add,
             )
 
-        def drop_whole_turns(unit, tokens=ALL):
+        def round_bank(unit, t):
+            j = (unit % PASSES) * PACK + t
+            nc.vector.tensor_scalar(
+                out=whole_of(unit)[:, t, :], in0=acc[(unit, t)][:], scalar1=1.0 / TWO_PI,
+                scalar2=turn_bias[:, j : j + 1], op0=ALU.mult, op1=ALU.add,
+            )
+
+        def reduce_bank(unit, t):
+            if t == 0:
+                angle[unit] = wave.tile([P, PACK, CHUNK], F32, tag="angle", name="angle")
             nc.vector.scalar_tensor_tensor(
-                out=turns[unit][:, :, tokens], in0=turns[unit][:, :, tokens],
-                scalar=phase_turns[:, 0:1], in1=whole[unit][:, :, tokens],
-                op0=ALU.add, op1=ALU.subtract,
+                out=angle[unit][:, t, :], in0=whole[unit][:, t, :], scalar=-TWO_PI,
+                in1=acc[(unit, t)][:], op0=ALU.mult, op1=ALU.add,
             )
 
-        def sine(unit, tokens=ALL):
+        def sine_bank(unit, t):
+            j = (unit % PASSES) * PACK + t
             nc.scalar.activation(
-                out=turns[unit][:, :, tokens], in_=turns[unit][:, :, tokens], func=ACT.Sin, scale=TWO_PI
+                out=angle[unit][:, t, :], in_=angle[unit][:, t, :], func=ACT.Sin,
+                bias=angle_bias[:, j : j + 1], scale=1.0,
             )
 
-        def gain(unit, tokens=ALL, on_scalar=False):
-            if unit not in h2_grouped:
-                h2_grouped[unit] = stage.tile([P, CHUNK, PACK], BF16, tag="h2_grouped", name="h2_grouped", align_bytes=64)
-            if on_scalar:
-                nc.scalar.activation(
-                    out=h2_grouped[unit][:, tokens, :].rearrange("p (n i) t -> p n t i", i=4),
-                    in_=turns[unit][:, :, tokens].rearrange("p t (n i) -> p n t i", i=4),
-                    func=ACT.Copy, scale=amp[:, 0:1],
-                )
-            else:
-                nc.vector.tensor_scalar(
-                    out=h2_grouped[unit][:, tokens, :].rearrange("p (n i) t -> p n t i", i=4),
-                    in0=turns[unit][:, :, tokens].rearrange("p t (n i) -> p n t i", i=4),
-                    scalar1=amp[:, 0:1], scalar2=None, op0=ALU.mult,
-                )
+        def hand_ports_over(unit):
+            amp_now[unit] = wave.tile([P, 1], F32, tag="amp_now", name="amp_now", bufs=2)
+            nc.vector.tensor_copy(out=amp_now[unit][:], in_=amp[:])
+
+        def gain(unit):
+            h2_grouped[unit] = stage.tile([P, CHUNK, PACK], BF16, tag="h2_grouped", name="h2_grouped", align_bytes=64)
+            nc.gpsimd.tensor_scalar(
+                out=h2_grouped[unit][:], in0=angle[unit][:].rearrange("p t n -> p n t"),
+                scalar1=amp_now[unit][:, 0:1], scalar2=0.0, op0=ALU.mult, op1=ALU.add,
+            )
 
         def quantise_h2(unit, tokens=ALL):
             c, g2 = divmod(unit, PASSES)
@@ -404,7 +416,6 @@ def tile_transreachencoderlayer_pb_t_kernel(
         b2_bank = banks.tile([P, 2, 2 * P], F32, tag="bank", name="bank")
         b2_words = keep.tile([P, FEATURE_TILES // 2], F32)
         b2_cols = keep.tile([P, FEATURE_TILES], F32)
-        b2_turns = keep.tile([P, FEATURE_TILES], F32)
         by_scalar = nc.scalar.copy
         by_vector = nc.vector.tensor_copy
         deal(6)
@@ -466,7 +477,6 @@ def tile_transreachencoderlayer_pb_t_kernel(
         turns_bank(0, 2)
         deal(1)
         quantise_w2(5)
-        turns_bank(0, 3)
         turn_w2(6)
         turn_w2(7)
         turn_h1(2, 0)
@@ -475,7 +485,7 @@ def tile_transreachencoderlayer_pb_t_kernel(
         turn_h1(2, 2)
         lay_w2(by_scalar, 7)
         turn_h1(3, 0)
-        nearest_whole_turns(0)
+        round_turns(0)
         lay_h1(by_scalar, 2, 0)
         turn_h1(3, 2)
         quantise_w2(6)
@@ -483,80 +493,58 @@ def tile_transreachencoderlayer_pb_t_kernel(
         quantise_w2(7)
         deal(1)
         lay_h1(by_scalar, 2, 2)
-        for t in range(PACK):
-            matmul_bank(1, t)
-        drop_whole_turns(0)
         deal(1)
         lay_h1(by_vector, 3, 0)
         deal(1)
         lay_h1(by_vector, 3, 2)
         deal(len(small))
-        for t in range(PACK):
-            turns_bank(1, t)
         quantise_h1(2)
 
         def due(unit):
             return 0 <= unit < UNITS
 
-        for step in range(UNITS - 1):
+        for step in range(UNITS + 4):
             if due(step - 1):
-                sine(step - 1)
+                hand_ports_over(step - 1)
+                gain(step - 1)
+            if due(step):
+                for t in range(VIA_SCALAR, PACK):
+                    round_bank(step, t)
+            for t in range(PACK):
+                if due(step):
+                    reduce_bank(step, t)
+                if due(step + 1):
+                    matmul_bank(step + 1, t)
+            if due(step - 3):
+                second_add(step - 3)
+            if due(step):
+                sine_bank(step, 0)
+                sine_bank(step, 1)
+            if due(step + 1):
+                for t in range(VIA_SCALAR):
+                    turns_bank(step + 1, t)
+            if due(step):
+                sine_bank(step, 2)
+                sine_bank(step, 3)
             if step == 1 or step == 2:
                 turn_w3(step - 1)
-            if due(step + 1) and step > 0:
-                first_matmul(step + 1)
-            if due(step) and step > 0:
-                nearest_whole_turns(step)
-            if due(step + 3):
-                quantise_h1(step + 3)
-            elif due(step - 2):
-                quantise_h2(step - 2)
-            if due(step) and step > 0:
-                drop_whole_turns(step)
+                lay_w3(nc.vector.tensor_copy, step - 1)
             if due(step + 4):
                 group_h1(step + 4)
             if due(step):
                 residual_and_bias(step)
             if due(step - 1):
-                gain(step - 1)
+                quantise_h2(step - 1)
             if step == 1 or step == 2:
-                lay_w3(nc.vector.tensor_copy, step - 1)
-            if due(step + 3) and due(step - 2):
-                quantise_h2(step - 2)
-            if step == 2 or step == 3:
-                quantise_w3(step - 2)
-            if due(step - SECOND_LAG):
-                second_matmul(step - SECOND_LAG)
+                quantise_w3(step - 1)
+            if due(step - 2):
+                second_sums(step - 2)
+            if due(step + 3):
+                quantise_h1(step + 3)
+            if due(step + 1):
+                round_turns(step + 1)
             if step % 2 == 0:
                 if step // 2 + 4 < N_CHUNKS:
                     load_h1(step // 2 + 4, 1)
                 if step // 2 + 1 < N_CHUNKS:
                     load_x1(step // 2 + 1)
-
-        FIRST = slice(0, CHUNK // 2)
-        LAST = slice(CHUNK // 2, CHUNK)
-        sine(14)
-        nearest_whole_turns(15, FIRST)
-        nearest_whole_turns(15, LAST)
-        drop_whole_turns(15, FIRST)
-        quantise_h2(13)
-        drop_whole_turns(15, LAST)
-        residual_and_bias(15)
-        gain(14, ALL, True)
-        sine(15, FIRST)
-        sine(15, LAST)
-        second_sums(11)
-        second_add(11)
-        second_sums(12)
-        second_sums(13)
-        quantise_h2(14)
-        second_add(12)
-        gain(15, FIRST)
-        gain(15, LAST, True)
-        second_add(13)
-        quantise_h2(15, FIRST)
-        second_sums(14)
-        quantise_h2(15, LAST)
-        second_add(14)
-        second_sums(15)
-        second_add(15)

@@ -32,7 +32,7 @@ TINY = 1e-30
 SECOND_LAG = 4
 PHASE_STEPS = 3
 
-SPARE_BANKS_FROM_END = 0
+SPARE_BANKS_FROM_END = 3
 WARM_UP = 6
 VIA_SCALAR = 3
 
@@ -357,6 +357,16 @@ def tile_transreachencoderlayer_pb_t_kernel(
                 scalar1=amp_now[unit][:, 0:1], scalar2=0.0, op0=ALU.mult, op1=ALU.add,
             )
 
+        def gain_in_the_tail(unit, tokens, on_scalar):
+            if unit not in h2_grouped:
+                h2_grouped[unit] = stage.tile([P, CHUNK, PACK], BF16, tag="h2_grouped", name="h2_grouped", align_bytes=64)
+            laid = h2_grouped[unit][:, tokens, :].rearrange("p (n i) t -> p n t i", i=4)
+            sines = angle[unit][:, :, tokens].rearrange("p t (n i) -> p n t i", i=4)
+            if on_scalar:
+                nc.scalar.activation(out=laid, in_=sines, func=ACT.Copy, scale=amp[:, 0:1])
+            else:
+                nc.vector.tensor_scalar(out=laid, in0=sines, scalar1=amp[:, 0:1], scalar2=None, op0=ALU.mult)
+
         def quantise_h2(unit, tokens=ALL):
             c, g2 = divmod(unit, PASSES)
             if c not in h2_codes:
@@ -492,21 +502,17 @@ def tile_transreachencoderlayer_pb_t_kernel(
         deal(1)
         quantise_w2(7)
         deal(1)
+        deal(1)
         lay_h1(by_scalar, 2, 2)
+        lay_h1(by_scalar, 3, 0)
         deal(1)
-        lay_h1(by_vector, 3, 0)
-        deal(1)
-        lay_h1(by_vector, 3, 2)
-        deal(len(small))
-        quantise_h1(2)
 
         def due(unit):
             return 0 <= unit < UNITS
 
-        for step in range(UNITS + 4):
-            if due(step - 1):
-                hand_ports_over(step - 1)
-                gain(step - 1)
+        for step in range(UNITS):
+            if step == 1 or step == 2:
+                turn_w3(step - 1)
             if due(step):
                 for t in range(VIA_SCALAR, PACK):
                     round_bank(step, t)
@@ -515,6 +521,11 @@ def tile_transreachencoderlayer_pb_t_kernel(
                     reduce_bank(step, t)
                 if due(step + 1):
                     matmul_bank(step + 1, t)
+            if step == 0:
+                lay_h1(by_vector, 3, 2)
+                deal(len(small))
+            if step == 1 or step == 2:
+                lay_w3(by_vector, step - 1)
             if due(step - 3):
                 second_add(step - 3)
             if due(step):
@@ -526,25 +537,40 @@ def tile_transreachencoderlayer_pb_t_kernel(
             if due(step):
                 sine_bank(step, 2)
                 sine_bank(step, 3)
-            if step == 1 or step == 2:
-                turn_w3(step - 1)
-                lay_w3(nc.vector.tensor_copy, step - 1)
             if due(step + 4):
                 group_h1(step + 4)
             if due(step):
                 residual_and_bias(step)
             if due(step - 1):
                 quantise_h2(step - 1)
+            if step == 0:
+                quantise_h1(2)
             if step == 1 or step == 2:
                 quantise_w3(step - 1)
             if due(step - 2):
                 second_sums(step - 2)
             if due(step + 3):
                 quantise_h1(step + 3)
+            if due(step) and step + 1 < UNITS:
+                hand_ports_over(step)
             if due(step + 1):
                 round_turns(step + 1)
+            if due(step) and step + 1 < UNITS:
+                gain(step)
             if step % 2 == 0:
                 if step // 2 + 4 < N_CHUNKS:
                     load_h1(step // 2 + 4, 1)
                 if step // 2 + 1 < N_CHUNKS:
                     load_x1(step // 2 + 1)
+
+        FIRST = slice(0, CHUNK // 2)
+        LAST = slice(CHUNK // 2, CHUNK)
+        gain_in_the_tail(15, FIRST, False)
+        gain_in_the_tail(15, LAST, True)
+        second_add(13)
+        quantise_h2(15, FIRST)
+        second_sums(14)
+        quantise_h2(15, LAST)
+        second_sums(15)
+        second_add(14)
+        second_add(15)

@@ -461,56 +461,76 @@ def tile_transreachencoderlayer_pb_t_kernel(
         lay_w2(by_scalar, 1)
         deal(1)
         turn_w2(3)
-        keep_clock_up(1)
         quantise_w2(0)
         lay_w2(by_scalar, 2)
         deal(1)
-        turn_w2(4)
+        matmul_bank(0, 0)
         quantise_w2(1)
         lay_w2(by_scalar, 3)
         deal(1)
-        turn_w2(5)
-        keep_clock_up(1)
-        quantise_w2(2)
-        deal(1)
-        matmul_bank(0, 0)
-        quantise_w2(3)
         matmul_bank(0, 1)
-        lay_w2(by_vector, 4)
+        quantise_w2(2)
+        deal(2)
         turns_bank(0, 0)
         matmul_bank(0, 2)
-        lay_w2(by_vector, 5)
+        quantise_w2(3)
+        deal(1)
         turns_bank(0, 1)
         matmul_bank(0, 3)
-        deal(1)
-        quantise_w2(4)
+        turn_w2(4)
+        turn_w2(5)
         turns_bank(0, 2)
-        deal(1)
-        quantise_w2(5)
-        turn_w2(6)
-        turn_w2(7)
-        turn_h1(2, 0)
         deal(2)
-        lay_w2(by_scalar, 6)
-        turn_h1(2, 2)
-        lay_w2(by_scalar, 7)
-        turn_h1(3, 0)
+        turn_w2(6)
+        lay_w2(by_scalar, 4)
+        lay_w2(by_scalar, 5)
+        turn_w2(7)
         round_turns(0)
-        lay_h1(by_scalar, 2, 0)
-        turn_h1(3, 2)
-        quantise_w2(6)
         deal(1)
-        quantise_w2(7)
+        lay_w2(by_scalar, 6)
+        quantise_w2(4)
         deal(1)
+        lay_w2(by_scalar, 7)
+        turn_h1(2, 0)
+        turn_h1(2, 2)
+        round_bank(0, 3)
+        for t in range(PACK):
+            reduce_bank(0, t)
+            if t + 1 < PACK:
+                quantise_w2(PACK + t + 1)
+            matmul_bank(1, t)
+            if t == 0:
+                lay_h1(by_scalar, 2, 0)
+                turn_h1(3, 0)
+                deal(1)
+            if t == 1:
+                lay_h1(by_scalar, 2, 2)
+                turn_h1(3, 2)
+                deal(1)
+        sine_bank(0, 0)
+        sine_bank(0, 1)
+        for t in range(VIA_SCALAR):
+            turns_bank(1, t)
+        lay_h1(by_vector, 3, 0)
         deal(1)
-        lay_h1(by_scalar, 2, 2)
-        lay_h1(by_scalar, 3, 0)
-        deal(1)
+        lay_h1(by_vector, 3, 2)
+        deal(len(small))
+        sine_bank(0, 2)
+        sine_bank(0, 3)
+        group_h1(4)
+        residual_and_bias(0)
+        quantise_h1(2)
+        quantise_h1(3)
+        hand_ports_over(0)
+        round_turns(1)
+        gain(0)
+        load_h1(4, 1)
+        load_x1(1)
 
         def due(unit):
             return 0 <= unit < UNITS
 
-        for step in range(UNITS):
+        for step in range(1, UNITS):
             if step == 1 or step == 2:
                 turn_w3(step - 1)
             if due(step):
@@ -521,11 +541,8 @@ def tile_transreachencoderlayer_pb_t_kernel(
                     reduce_bank(step, t)
                 if due(step + 1):
                     matmul_bank(step + 1, t)
-            if step == 0:
-                lay_h1(by_vector, 3, 2)
-                deal(len(small))
             if step == 1 or step == 2:
-                lay_w3(by_vector, step - 1)
+                lay_w3(by_scalar if step == 1 else by_vector, step - 1)
             if due(step - 3):
                 second_add(step - 3)
             if due(step):
@@ -543,8 +560,6 @@ def tile_transreachencoderlayer_pb_t_kernel(
                 residual_and_bias(step)
             if due(step - 1):
                 quantise_h2(step - 1)
-            if step == 0:
-                quantise_h1(2)
             if step == 1 or step == 2:
                 quantise_w3(step - 1)
             if due(step - 2):

@@ -83,6 +83,19 @@ def tile_transreachencoderlayer_pb_t_kernel(
                 unread = u2_banks.tile([P, CHUNK], F32, tag="u2", name="u2")
                 nc.tensor.matmul(out=unread[:], lhsT=zeros[:, 0:P], rhs=zeros[:], start=True, stop=True)
 
+        def keep_clock_up_mx(count):
+            unread = banks.tile([P, CHUNK], F32, tag="bank", name="bank")
+            for repeat in range(count):
+                nc.tensor.matmul_mx(
+                    out=unread[:],
+                    lhsT=w2_codes[:, 0, 0:P].bitcast(FP8X4),
+                    lhsT_scale=w2_scales[:, 0, 0:P],
+                    rhs=w2_codes[:, 0:2, :].rearrange("p j n -> p (j n)").bitcast(FP8X4),
+                    rhs_scale=w2_scales[:, 0:2, :].rearrange("p j n -> p (j n)"),
+                    start=True,
+                    stop=True,
+                )
+
         keep_clock_up(WARM_UP)
         nc.vector.memset(warm[:], 0.0)
         nc.scalar.activation(out=warm[:], in_=warm[:], func=ACT.Sin)
@@ -564,6 +577,7 @@ def tile_transreachencoderlayer_pb_t_kernel(
                 quantise_w3(step - 1)
             if due(step - 2):
                 second_sums(step - 2)
+            keep_clock_up_mx(2)
             if due(step + 3):
                 quantise_h1(step + 3)
             if due(step) and step + 1 < UNITS:
@@ -580,6 +594,7 @@ def tile_transreachencoderlayer_pb_t_kernel(
 
         FIRST = slice(0, CHUNK // 2)
         LAST = slice(CHUNK // 2, CHUNK)
+        keep_clock_up_mx(6)
         gain_in_the_tail(15, FIRST, False)
         gain_in_the_tail(15, LAST, True)
         second_add(13)

@@ -83,8 +83,11 @@ def tile_transreachencoderlayer_pb_t_kernel(
                 unread = u2_banks.tile([P, CHUNK], F32, tag="u2", name="u2")
                 nc.tensor.matmul(out=unread[:], lhsT=zeros[:, 0:P], rhs=zeros[:], start=True, stop=True)
 
-        def keep_clock_up_mx(count):
-            unread = banks.tile([P, CHUNK], F32, tag="bank", name="bank")
+        def keep_clock_up_mx(count, in_the_head=False):
+            if in_the_head:
+                unread = out_banks.tile([P, CHUNK], F32, tag="acc2", name="acc2")
+            else:
+                unread = banks.tile([P, CHUNK], F32, tag="bank", name="bank")
             for repeat in range(count):
                 nc.tensor.matmul_mx(
                     out=unread[:],
@@ -450,12 +453,14 @@ def tile_transreachencoderlayer_pb_t_kernel(
         nc.vector.tensor_scalar(out=b2_turns[:], in0=b2_cols[:], scalar1=1.0 / TWO_PI, scalar2=None, op0=ALU.mult)
         deal(4)
         turn_h1(0, 0)
+        keep_clock_up(1)
         turn_h1(1, 0)
         keep_clock_up(1)
         lay_h1(by_scalar, 0, 0)
         deal(1)
         lay_h1(by_vector, 1, 0)
         turn_h1(0, 2)
+        keep_clock_up(1)
         turn_h1(1, 2)
         keep_clock_up(1)
         lay_h1(by_scalar, 0, 2)
@@ -464,16 +469,19 @@ def tile_transreachencoderlayer_pb_t_kernel(
         load_h1(3, 1)
         deal(1)
         turn_w2(0)
+        keep_clock_up(1)
         turn_w2(1)
         keep_clock_up(1)
         quantise_h1(0)
         lay_w2(by_scalar, 0)
         deal(1)
         turn_w2(2)
+        keep_clock_up(1)
         quantise_h1(1)
         lay_w2(by_scalar, 1)
         deal(1)
         turn_w2(3)
+        keep_clock_up(1)
         quantise_w2(0)
         lay_w2(by_scalar, 2)
         deal(1)
@@ -492,12 +500,14 @@ def tile_transreachencoderlayer_pb_t_kernel(
         matmul_bank(0, 3)
         turn_w2(4)
         turn_w2(5)
+        keep_clock_up_mx(1, True)
         turns_bank(0, 2)
         deal(2)
         turn_w2(6)
         lay_w2(by_scalar, 4)
         lay_w2(by_scalar, 5)
         turn_w2(7)
+        keep_clock_up_mx(1, True)
         round_turns(0)
         deal(1)
         lay_w2(by_scalar, 6)
@@ -506,6 +516,7 @@ def tile_transreachencoderlayer_pb_t_kernel(
         lay_w2(by_scalar, 7)
         turn_h1(2, 0)
         turn_h1(2, 2)
+        keep_clock_up_mx(1, True)
         round_bank(0, 3)
         for t in range(PACK):
             reduce_bank(0, t)
@@ -532,6 +543,7 @@ def tile_transreachencoderlayer_pb_t_kernel(
         sine_bank(0, 3)
         group_h1(4)
         residual_and_bias(0)
+        keep_clock_up_mx(2, True)
         quantise_h1(2)
         quantise_h1(3)
         hand_ports_over(0)

import math
from contextlib import ExitStack

import concourse.mybir as mybir
from concourse.masks import make_identity

F32 = mybir.dt.float32
BF16 = mybir.dt.bfloat16
U32 = mybir.dt.uint32
I32 = mybir.dt.int32
U8 = mybir.dt.uint8
FP8X4 = mybir.dt.float8_e4m3fn_x4
ALU = mybir.AluOpType
ACT = mybir.ActivationFunctionType

P = 128
PACK = 4
TOKENS = 4 * 1024
HIDDEN = 1024
MODEL = 256
PASSES = HIDDEN // (P * PACK)
WORDS = P * PACK // 2
CHUNK = 512
ROW_TILES = CHUNK // P
FEATURE_TILES = HIDDEN // P
N_CHUNKS = TOKENS // CHUNK
UNITS = 2 * N_CHUNKS

TWO_PI = 2.0 * math.pi
ROUND_MAGIC = 1.5 * 2.0**23
TINY = 1e-30
SECOND_LAG = 4
PHASE_STEPS = 3

SPARE_BANKS_FROM_END = 3
WARM_UP = 6
VIA_SCALAR = 3

FLOPS = 2 * TOKENS * HIDDEN * HIDDEN + 2 * TOKENS * HIDDEN * MODEL


def tile_transreachencoderlayer_pb_t_kernel(
    tc, h1, x1, ffn_w2, ffn_b2, ffn_a2w1, ffn_a2w2, ffn_w3, ffn_b3, out
):
    nc = tc.nc
    h1_chunks = h1.flatten_outer_dims().rearrange("(c p i) k -> c p i k", p=P, i=ROW_TILES)
    x1_chunks = x1.flatten_outer_dims().rearrange("(c p i) d -> c p i d", p=P, i=ROW_TILES)
    out_chunks = out.flatten_outer_dims().rearrange("(c p i) d -> c p i d", p=P, i=ROW_TILES)

    with ExitStack() as pools:
        keep = pools.enter_context(tc.tile_pool(name="keep", bufs=1))
        stage = pools.enter_context(tc.tile_pool(name="stage", bufs=3))
        loads = pools.enter_context(tc.tile_pool(name="loads", bufs=3))
        wave = pools.enter_context(tc.tile_pool(name="wave", bufs=3))
        banks = pools.enter_context(tc.psum_pool(name="banks", bufs=3))
        u2_banks = pools.enter_context(tc.psum_pool(name="u2_banks", bufs=PACK))
        out_banks = pools.enter_context(tc.psum_pool(name="out_banks", bufs=1))
        pools.enter_context(tc.manual_schedule())

        warm = keep.tile([P, 1], F32)
        w1_bf = keep.tile([P, 1], BF16)
        w2_bf = keep.tile([P, 1], BF16)
        minus_half = keep.tile([P, 1], F32)
        b2_rows = keep.tile([P, 2 * P], BF16)
        b3_row = keep.tile([P, MODEL], BF16)
        first_row = keep.tile([P, P], BF16)
        identity = keep.tile([P, P], F32)
        identity_bf = keep.tile([P, P], BF16)
        w2_raw = keep.tile([P, FEATURE_TILES, HIDDEN], BF16)
        w3_raw = keep.tile([P, MODEL // P, HIDDEN], BF16)
        w2_codes = keep.tile([P, FEATURE_TILES, PASSES * P], U32, align_bytes=64)
        w2_scales = keep.tile([P, FEATURE_TILES, PASSES * P], U8, align_bytes=64)
        w3_codes = keep.tile([P, PASSES, MODEL], U32, align_bytes=64)
        w3_scales = keep.tile([P, PASSES, MODEL], U8, align_bytes=64)
        h1_raw = {}
        x1_raw = {}

        zeros = keep.tile([P, CHUNK], BF16)
        nc.vector.memset(zeros[:], 0.0)

        def keep_clock_up(count):
            for repeat in range(count):
                unread = u2_banks.tile([P, CHUNK], F32, tag="u2", name="u2")
                nc.tensor.matmul(out=unread[:], lhsT=zeros[:, 0:P], rhs=zeros[:], start=True, stop=True)

        def keep_clock_up_mx(count, in_the_head=False):
            if in_the_head:
                unread = out_banks.tile([P, CHUNK], F32, tag="acc2", name="acc2")
            else:
                unread = banks.tile([P, CHUNK], F32, tag="bank", name="bank")
            for repeat in range(count):
                nc.tensor.matmul_mx(
                    out=unread[:],
                    lhsT=w2_codes[:, 0, 0:P].bitcast(FP8X4),
                    lhsT_scale=w2_scales[:, 0, 0:P],
                    rhs=w2_codes[:, 0:2, :].rearrange("p j n -> p (j n)").bitcast(FP8X4),
                    rhs_scale=w2_scales[:, 0:2, :].rearrange("p j n -> p (j n)"),
                    start=True,
                    stop=True,
                )

        keep_clock_up(WARM_UP)
        nc.vector.memset(warm[:], 0.0)
        nc.scalar.activation(out=warm[:], in_=warm[:], func=ACT.Sin)
        nc.vector.memset(b2_rows[:], 0.0)
        make_identity(nc, identity[:])
        make_identity(nc, identity_bf[:])

        def load_w2(g, u):
            j = g * PACK + 2 * u
            r0 = (g * PACK + 2 * u) * P
            nc.sync.dma_start(
                out=w2_raw[:, j : j + 2, :].rearrange("m e k -> m (e k)"),
                in_=ffn_w2[r0 : r0 + 2 * P, :].rearrange("(m e) k -> m (e k)", e=2),
            )

        def load_h1(c, pieces):
            h1_raw[c] = loads.tile([P, ROW_TILES, HIDDEN], BF16, tag="h1_raw", name="h1_raw")
            n = ROW_TILES // pieces
            for piece in range(pieces):
                rows = slice(piece * n, (piece + 1) * n)
                nc.sync.dma_start(out=h1_raw[c][:, rows, :], in_=h1_chunks[c][:, rows, :])

        def load_x1(c):
            x1_raw[c] = loads.tile([P, ROW_TILES, MODEL], BF16, tag="x1_raw", name="x1_raw")
            nc.sync.dma_start(out=x1_raw[c][:], in_=x1_chunks[c])

        nc.sync.dma_start(out=w1_bf[:], in_=ffn_a2w1.partition_broadcast(P))
        nc.sync.dma_start(out=w2_bf[:], in_=ffn_a2w2.partition_broadcast(P))
        nc.sync.dma_start(
            out=b2_rows[0 : FEATURE_TILES // 2, :],
            in_=ffn_b2.rearrange("(a w) -> a w", a=FEATURE_TILES // 2),
        )
        load_h1(0, 2)
        load_w2(0, 0)
        load_w2(0, 1)
        load_w2(1, 0)
        load_w2(1, 1)
        load_h1(1, 1)
        nc.vector.memset(minus_half[:], -0.5)
        nc.vector.memset(b3_row[:], 0.0)
        nc.vector.memset(first_row[:], 0.0)
        nc.vector.memset(first_row[0:1, :], 1.0)
        nc.sync.dma_start(out=b3_row[0:1, :], in_=ffn_b3.rearrange("(o d) -> o d", o=1))
        load_x1(0)
        nc.sync.dma_start(out=w3_raw[:], in_=ffn_w3.rearrange("(i p) k -> p i k", p=P))
        load_h1(2, 1)

        gains = keep.tile([P, 2], F32)
        w1_sq = keep.tile([P, 1], F32)
        amp_sq = keep.tile([P, 1], F32)
        inv_amp = keep.tile([P, 1], F32)
        half = keep.tile([P, 1], F32)
        coef = keep.tile([P, 1], F32)
        ab = keep.tile([P, 2], F32)
        angles = keep.tile([P, 2], F32)
        cos_sin = keep.tile([P, 2], F32)
        partial = keep.tile([P, 1], F32)
        quarter_turn = keep.tile([P, 1], F32)
        phase_turns = keep.tile([P, 1], F32)
        signed = keep.tile([P, 2], F32)
        w1_part = keep.tile([P, 1], F32)
        amp = keep.tile([P, 1], F32)
        b2_turns = keep.tile([P, FEATURE_TILES], F32)
        turn_bias = keep.tile([P, FEATURE_TILES], F32)
        angle_bias = keep.tile([P, FEATURE_TILES], F32)
        psi = angles[:, 1:2]
        ts = nc.vector.tensor_scalar

        small = [
            lambda: nc.vector.tensor_copy(out=gains[:, 0:1], in_=w1_bf[:]),
            lambda: nc.vector.tensor_copy(out=gains[:, 1:2], in_=w2_bf[:]),
            lambda: ts(out=w1_sq[:], in0=gains[:, 0:1], scalar1=gains[:, 0:1], scalar2=TINY, op0=ALU.mult, op1=ALU.add),
            lambda: ts(out=half[:], in0=gains[:, 1:2], scalar1=0.0, scalar2=0.5, op0=ALU.is_ge, op1=ALU.subtract),
            lambda: ts(out=amp_sq[:], in0=gains[:, 1:2], scalar1=gains[:, 1:2], scalar2=w1_sq[:, 0:1], op0=ALU.mult, op1=ALU.add),
            lambda: nc.gpsimd.tensor_tensor(out=inv_amp[:], in0=amp_sq[:], in1=minus_half[:], op=ALU.pow),
            lambda: ts(out=quarter_turn[:], in0=half[:], scalar1=0.5, scalar2=None, op0=ALU.mult),
            lambda: ts(out=signed[:], in0=gains[:], scalar1=half[:, 0:1], scalar2=2.0, op0=ALU.mult, op1=ALU.mult),
            lambda: ts(out=coef[:], in0=half[:], scalar1=-2.0, scalar2=inv_amp[:, 0:1], op0=ALU.mult, op1=ALU.mult),
            lambda: ts(out=ab[:], in0=gains[:], scalar1=coef[:, 0:1], scalar2=None, op0=ALU.mult),
            lambda: nc.vector.tensor_copy(out=psi, in_=ab[:, 0:1]),
        ]
        cos_and_sin_of_psi = [
            lambda: ts(out=angles[:, 0:1], in0=psi, scalar1=0.5 * math.pi, scalar2=None, op0=ALU.add),
            lambda: nc.scalar.activation(out=cos_sin[:], in_=angles[:], func=ACT.Sin),
        ]
        for repeat in range(PHASE_STEPS):
            small.extend(cos_and_sin_of_psi)
            small.extend([
                lambda: ts(out=partial[:], in0=cos_sin[:, 0:1], scalar1=ab[:, 0:1], scalar2=psi, op0=ALU.mult, op1=ALU.add),
                lambda: ts(out=psi, in0=cos_sin[:, 1:2], scalar1=ab[:, 1:2], scalar2=partial[:, 0:1], op0=ALU.mult, op1=ALU.add),
            ])
        small.append(
            lambda: ts(out=phase_turns[:], in0=psi, scalar1=1.0 / TWO_PI, scalar2=quarter_turn[:, 0:1], op0=ALU.mult, op1=ALU.add)
        )
        small.extend([
            lambda: ts(out=turn_bias[:], in0=b2_turns[:], scalar1=phase_turns[:, 0:1], scalar2=None, op0=ALU.add),
            lambda: ts(out=angle_bias[:], in0=turn_bias[:], scalar1=TWO_PI, scalar2=None, op0=ALU.mult),
        ])
        small.extend(cos_and_sin_of_psi)
        small.extend([
            lambda: ts(out=w1_part[:], in0=cos_sin[:, 1:2], scalar1=signed[:, 0:1], scalar2=None, op0=ALU.mult),
            lambda: ts(out=amp[:], in0=cos_sin[:, 0:1], scalar1=signed[:, 1:2], scalar2=w1_part[:, 0:1], op0=ALU.mult, op1=ALU.subtract),
        ])
        dealt = [0]

        def deal(count):
            for repeat in range(count):
                if dealt[0] < len(small):
                    small[dealt[0]]()
                    dealt[0] += 1

        def turn_rows(rows, first, g):
            words = rows.bitcast(F32)
            bank = banks.tile([P, 2, 2 * P], F32, tag="bank", name="bank")
            for u in range(2):
                for i in range(2):
                    w0 = g * WORDS + u * P
                    nc.tensor.transpose(
                        out=bank[:, u, i * P : (i + 1) * P], in_=words[:, first + i, w0 : w0 + P],
                        identity=identity[:],
                    )
            return bank

        def lay_rows(copy, grouped, first, bank):
            pairs = grouped.bitcast(F32).rearrange("p (r u) -> p r u", u=2)
            copy(out=pairs[:, first * P : (first + 2) * P, :], in_=bank[:].rearrange("p u r -> p r u"))

        w2_bank = {}
        w2_grouped = {}

        def turn_w2(j):
            words = w2_raw[:].bitcast(F32)
            w2_bank[j] = banks.tile([P, PASSES, 2, P], F32, tag="bank", name="bank")
            for g in range(PASSES):
                for u in range(2):
                    w0 = g * WORDS + u * P
                    nc.tensor.transpose(
                        out=w2_bank[j][:, g, u, :], in_=words[:, j, w0 : w0 + P], identity=identity[:]
                    )

        def lay_w2(copy, j):
            w2_grouped[j] = stage.tile([P, PASSES * P * PACK], BF16, tag="w2_grouped", name="w2_grouped", align_bytes=64)
            copy(
                out=w2_grouped[j][:].bitcast(F32).rearrange("p (g r u) -> p g r u", g=PASSES, u=2),
                in_=w2_bank[j][:].rearrange("p g u r -> p g r u"),
            )

        def quantise_w2(j):
            nc.vector.quantize_mx(
                out=w2_codes[:, j, :].bitcast(FP8X4), scales=w2_scales[:, j, :], in_=w2_grouped[j][:]
            )

        w3_bank = {}
        w3_grouped = {}

        def turn_w3(g):
            w3_bank[g] = turn_rows(w3_raw[:], 0, g)

        def lay_w3(copy, g):
            w3_grouped[g] = stage.tile([P, MODEL * PACK], BF16, tag="w3_grouped", name="w3_grouped", align_bytes=64)
            lay_rows(copy, w3_grouped[g][:], 0, w3_bank[g])

        def quantise_w3(g):
            nc.vector.quantize_mx(
                out=w3_codes[:, g, :].bitcast(FP8X4), scales=w3_scales[:, g, :], in_=w3_grouped[g][:]
            )

        h1_bank = {}
        h1_grouped = {}
        h1_codes = {}
        h1_scales = {}
        acc = {}
        turns = {}
        whole = {}
        h2_grouped = {}
        h2_codes = {}
        h2_scales = {}
        residual = {}

        def turn_h1(unit, first):
            c, g = divmod(unit, PASSES)
            h1_bank[(unit, first)] = turn_rows(h1_raw[c][:], first, g)

        def lay_h1(copy, unit, first):
            if unit not in h1_grouped:
                h1_grouped[unit] = stage.tile([P, CHUNK * PACK], BF16, tag="h1_grouped", name="h1_grouped", align_bytes=64)
            lay_rows(copy, h1_grouped[unit][:], first, h1_bank[(unit, first)])

        def group_h1(unit):
            for first in range(0, ROW_TILES, 2):
                turn_h1(unit, first)
                lay_h1(nc.scalar.copy, unit, first)

        def quantise_h1(unit):
            c, g = divmod(unit, PASSES)
            if g == 0:
                h1_codes[c] = stage.tile([P, PASSES, CHUNK], U32, tag="h1_codes", name="h1_codes", align_bytes=64)
                h1_scales[c] = stage.tile([P, PASSES, CHUNK], U8, tag="h1_scales", name="h1_scales", align_bytes=64)
            nc.vector.quantize_mx(
                out=h1_codes[c][:, g, :].bitcast(FP8X4), scales=h1_scales[c][:, g, :], in_=h1_grouped[unit][:]
            )

        def matmul_bank(unit, t):
            c, g2 = divmod(unit, PASSES)
            j = g2 * PACK + t
            acc[(unit, t)] = u2_banks.tile([P, CHUNK], F32, tag="u2", name="u2")
            for g in range(PASSES):
                nc.tensor.matmul_mx(
                    out=acc[(unit, t)][:],
                    lhsT=w2_codes[:, j, g * P : (g + 1) * P].bitcast(FP8X4),
                    lhsT_scale=w2_scales[:, j, g * P : (g + 1) * P],
                    rhs=h1_codes[c][:, g, :].bitcast(FP8X4),
                    rhs_scale=h1_scales[c][:, g, :],
                    start=(g == 0),
                    stop=(g == PASSES - 1),
                )

        ALL = slice(0, CHUNK)
        angle = {}
        amp_now = {}

        def turns_bank(unit, t):
            j = (unit % PASSES) * PACK + t
            if t == 0:
                turns[unit] = wave.tile([P, VIA_SCALAR, CHUNK], F32, tag="turns", name="turns", bufs=2)
            nc.scalar.activation(
                out=turns[unit][:, t, :], in_=acc[(unit, t)][:], func=ACT.Identity,
                bias=b2_turns[:, j : j + 1], scale=1.0 / TWO_PI,
            )

        def whole_of(unit):
            if unit not in whole:
                whole[unit] = wave.tile([P, PACK, CHUNK], I32, tag="whole", name="whole", bufs=2)
            return whole[unit]

        def round_turns(unit):
            nc.vector.tensor_scalar(
                out=whole_of(unit)[:, 0:VIA_SCALAR, :], in0=turns[unit][:], scalar1=phase_turns[:, 0:1],
                scalar2=None, op0=ALU.add,
            )

        def round_bank(unit, t):
            j = (unit % PASSES) * PACK + t
            nc.vector.tensor_scalar(
                out=whole_of(unit)[:, t, :], in0=acc[(unit, t)][:], scalar1=1.0 / TWO_PI,
                scalar2=turn_bias[:, j : j + 1], op0=ALU.mult, op1=ALU.add,
            )

        def reduce_bank(unit, t):
            if t == 0:
                angle[unit] = wave.tile([P, PACK, CHUNK], F32, tag="angle", name="angle")
            nc.vector.scalar_tensor_tensor(
                out=angle[unit][:, t, :], in0=whole[unit][:, t, :], scalar=-TWO_PI,
                in1=acc[(unit, t)][:], op0=ALU.mult, op1=ALU.add,
            )

        def sine_bank(unit, t):
            j = (unit % PASSES) * PACK + t
            nc.scalar.activation(
                out=angle[unit][:, t, :], in_=angle[unit][:, t, :], func=ACT.Sin,
                bias=angle_bias[:, j : j + 1], scale=1.0,
            )

        def hand_ports_over(unit):
            amp_now[unit] = wave.tile([P, 1], F32, tag="amp_now", name="amp_now", bufs=2)
            nc.vector.tensor_copy(out=amp_now[unit][:], in_=amp[:])

        def gain(unit):
            h2_grouped[unit] = stage.tile([P, CHUNK, PACK], BF16, tag="h2_grouped", name="h2_grouped", align_bytes=64)
            nc.gpsimd.tensor_scalar(
                out=h2_grouped[unit][:], in0=angle[unit][:].rearrange("p t n -> p n t"),
                scalar1=amp_now[unit][:, 0:1], scalar2=0.0, op0=ALU.mult, op1=ALU.add,
            )

        def gain_in_the_tail(unit, tokens, on_scalar):
            if unit not in h2_grouped:
                h2_grouped[unit] = stage.tile([P, CHUNK, PACK], BF16, tag="h2_grouped", name="h2_grouped", align_bytes=64)
            laid = h2_grouped[unit][:, tokens, :].rearrange("p (n i) t -> p n t i", i=4)
            sines = angle[unit][:, :, tokens].rearrange("p t (n i) -> p n t i", i=4)
            if on_scalar:
                nc.scalar.activation(out=laid, in_=sines, func=ACT.Copy, scale=amp[:, 0:1])
            else:
                nc.vector.tensor_scalar(out=laid, in0=sines, scalar1=amp[:, 0:1], scalar2=None, op0=ALU.mult)

        def quantise_h2(unit, tokens=ALL):
            c, g2 = divmod(unit, PASSES)
            if c not in h2_codes:
                h2_codes[c] = stage.tile([P, PASSES, CHUNK], U32, tag="h2_codes", name="h2_codes", align_bytes=64)
                h2_scales[c] = stage.tile([P, PASSES, CHUNK], U8, tag="h2_scales", name="h2_scales", align_bytes=64)
            nc.vector.quantize_mx(
                out=h2_codes[c][:, g2, tokens].bitcast(FP8X4), scales=h2_scales[c][:, g2, tokens],
                in_=h2_grouped[unit][:, tokens, :].rearrange("p n t -> p (n t)"),
            )

        def residual_and_bias(unit):
            c, first = unit // 2, 2 * (unit % 2)
            residual[unit] = loads.tile([P, 2, MODEL], F32, tag="residual", name="residual", bufs=SECOND_LAG + 1)
            bank = banks.tile([P, 2, MODEL], F32, tag="bank", name="bank")
            for i in range(2):
                nc.tensor.matmul(
                    out=bank[:, i, :], lhsT=identity_bf[:], rhs=x1_raw[c][:, first + i, :],
                    start=True, stop=False,
                )
                nc.tensor.matmul(
                    out=bank[:, i, :], lhsT=first_row[:], rhs=b3_row[:], start=False, stop=True
                )
            nc.scalar.copy(out=residual[unit][:], in_=bank[:])

        sums = {}

        def second_sums(unit):
            c, first = unit // 2, 2 * (unit % 2)
            if unit + SPARE_BANKS_FROM_END >= UNITS:
                acc2 = banks.tile([P, 2, MODEL], F32, tag="bank", name="bank")
            else:
                acc2 = out_banks.tile([P, 2, MODEL], F32, tag="acc2", name="acc2")
            sums[unit] = acc2
            for i in range(2):
                tok = slice((first + i) * P, (first + i + 1) * P)
                for g2 in range(PASSES):
                    nc.tensor.matmul_mx(
                        out=acc2[:, i, :],
                        lhsT=h2_codes[c][:, g2, tok].bitcast(FP8X4),
                        lhsT_scale=h2_scales[c][:, g2, tok],
                        rhs=w3_codes[:, g2, :].bitcast(FP8X4),
                        rhs_scale=w3_scales[:, g2, :],
                        start=(g2 == 0),
                        stop=(g2 == PASSES - 1),
                    )

        def second_add(unit):
            c, first = unit // 2, 2 * (unit % 2)
            result = loads.tile([P, 2, MODEL], F32, tag="result", name="result")
            nc.vector.tensor_tensor(out=result[:], in0=sums[unit][:], in1=residual[unit][:], op=ALU.add)
            nc.sync.dma_start(out=out_chunks[c][:, first : first + 2, :], in_=result[:])

        def second_matmul(unit):
            second_sums(unit)
            second_add(unit)

        b2_bank = banks.tile([P, 2, 2 * P], F32, tag="bank", name="bank")
        b2_words = keep.tile([P, FEATURE_TILES // 2], F32)
        b2_cols = keep.tile([P, FEATURE_TILES], F32)
        by_scalar = nc.scalar.copy
        by_vector = nc.vector.tensor_copy
        deal(6)
        nc.tensor.transpose(out=b2_bank[:, 0, 0:P], in_=b2_rows[:].bitcast(F32), identity=identity[:])
        nc.vector.tensor_copy(out=b2_words[:], in_=b2_bank[:, 0, 0 : FEATURE_TILES // 2])
        deal(1)
        nc.vector.tensor_copy(out=b2_cols[:], in_=b2_words[:].bitcast(BF16))
        deal(1)
        nc.vector.tensor_scalar(out=b2_turns[:], in0=b2_cols[:], scalar1=1.0 / TWO_PI, scalar2=None, op0=ALU.mult)
        deal(4)
        turn_h1(0, 0)
        keep_clock_up(1)
        turn_h1(1, 0)
        keep_clock_up(1)
        lay_h1(by_scalar, 0, 0)
        deal(1)
        lay_h1(by_vector, 1, 0)
        turn_h1(0, 2)
        keep_clock_up(1)
        turn_h1(1, 2)
        keep_clock_up(1)
        lay_h1(by_scalar, 0, 2)
        deal(1)
        lay_h1(by_vector, 1, 2)
        load_h1(3, 1)
        deal(1)
        turn_w2(0)
        keep_clock_up(1)
        turn_w2(1)
        keep_clock_up(1)
        quantise_h1(0)
        lay_w2(by_scalar, 0)
        deal(1)
        turn_w2(2)
        keep_clock_up(1)
        quantise_h1(1)
        lay_w2(by_scalar, 1)
        deal(1)
        turn_w2(3)
        keep_clock_up(1)
        quantise_w2(0)
        lay_w2(by_scalar, 2)
        deal(1)
        matmul_bank(0, 0)
        quantise_w2(1)
        lay_w2(by_scalar, 3)
        deal(1)
        matmul_bank(0, 1)
        quantise_w2(2)
        deal(2)
        turns_bank(0, 0)
        matmul_bank(0, 2)
        quantise_w2(3)
        deal(1)
        turns_bank(0, 1)
        matmul_bank(0, 3)
        turn_w2(4)
        turn_w2(5)
        keep_clock_up_mx(1, True)
        turns_bank(0, 2)
        deal(2)
        turn_w2(6)
        lay_w2(by_scalar, 4)
        lay_w2(by_scalar, 5)
        turn_w2(7)
        keep_clock_up_mx(1, True)
        round_turns(0)
        deal(1)
        lay_w2(by_scalar, 6)
        quantise_w2(4)
        deal(1)
        lay_w2(by_scalar, 7)
        turn_h1(2, 0)
        turn_h1(2, 2)
        keep_clock_up_mx(1, True)
        round_bank(0, 3)
        for t in range(PACK):
            reduce_bank(0, t)
            if t + 1 < PACK:
                quantise_w2(PACK + t + 1)
            matmul_bank(1, t)
            if t == 0:
                lay_h1(by_scalar, 2, 0)
                turn_h1(3, 0)
                deal(1)
            if t == 1:
                lay_h1(by_scalar, 2, 2)
                turn_h1(3, 2)
                deal(1)
        sine_bank(0, 0)
        sine_bank(0, 1)
        for t in range(VIA_SCALAR):
            turns_bank(1, t)
        lay_h1(by_vector, 3, 0)
        deal(1)
        lay_h1(by_vector, 3, 2)
        deal(len(small))
        sine_bank(0, 2)
        sine_bank(0, 3)
        group_h1(4)
        residual_and_bias(0)
        keep_clock_up_mx(2, True)
        quantise_h1(2)
        quantise_h1(3)
        hand_ports_over(0)
        round_turns(1)
        gain(0)
        load_h1(4, 1)
        load_x1(1)

        def due(unit):
            return 0 <= unit < UNITS

        for step in range(1, UNITS):
            if step == 1 or step == 2:
                turn_w3(step - 1)
            if due(step):
                for t in range(VIA_SCALAR, PACK):
                    round_bank(step, t)
            for t in range(PACK):
                if due(step):
                    reduce_bank(step, t)
                if due(step + 1):
                    matmul_bank(step + 1, t)
            if step == 1 or step == 2:
                lay_w3(by_scalar if step == 1 else by_vector, step - 1)
            if due(step - 3):
                second_add(step - 3)
            if due(step):
                sine_bank(step, 0)
                sine_bank(step, 1)
            if due(step + 1):
                for t in range(VIA_SCALAR):
                    turns_bank(step + 1, t)
            if due(step):
                sine_bank(step, 2)
                sine_bank(step, 3)
            if due(step + 4):
                group_h1(step + 4)
            if due(step):
                residual_and_bias(step)
            if due(step - 1):
                quantise_h2(step - 1)
            if step == 1 or step == 2:
                quantise_w3(step - 1)
            if due(step - 2):
                second_sums(step - 2)
            keep_clock_up_mx(2)
            if due(step + 3):
                quantise_h1(step + 3)
            if due(step) and step + 1 < UNITS:
                hand_ports_over(step)
            if due(step + 1):
                round_turns(step + 1)
            if due(step) and step + 1 < UNITS:
                gain(step)
            if step % 2 == 0:
                if step // 2 + 4 < N_CHUNKS:
                    load_h1(step // 2 + 4, 1)
                if step // 2 + 1 < N_CHUNKS:
                    load_x1(step // 2 + 1)

        FIRST = slice(0, CHUNK // 2)
        LAST = slice(CHUNK // 2, CHUNK)
        keep_clock_up_mx(6)
        gain_in_the_tail(15, FIRST, False)
        gain_in_the_tail(15, LAST, True)
        second_add(13)
        quantise_h2(15, FIRST)
        second_sums(14)
        quantise_h2(15, LAST)
        second_sums(15)
        second_add(14)
        second_add(15)
